import numpy as np
import ml_dtypes


def mxq(x, axis, fmt="e4m3"):
    dtype, down = {"e4m3": (ml_dtypes.float8_e4m3fn, 7), "e5m2": (ml_dtypes.float8_e5m2, 14)}[fmt]
    v = np.moveaxis(np.asarray(x, np.float32).astype(ml_dtypes.bfloat16).astype(np.float64), axis, -1)
    blocks = v.reshape(v.shape[:-1] + (-1, 32))
    amax = np.abs(blocks).max(-1, keepdims=True)
    byte = np.maximum(np.where(amax > 0, np.frexp(amax)[1] - 1 + 127, 0) - down, 1)
    scale = np.exp2(byte - 127.0)
    codes = (blocks / scale).astype(np.float32).astype(dtype).astype(np.float64)
    return np.moveaxis((codes * scale).reshape(v.shape), -1, axis)


WIDE = False


def mx_kscale(k):
    if not WIDE:
        return np.ones(k)
    levels = np.array([10, -10, 5, -5, 0])
    if k % 512:
        return np.exp2(np.random.permutation(np.resize(levels, k // 32))).repeat(32)
    a = np.empty((k // 512, 16))
    for p in range(k // 512):
        a[p, :8] = np.random.permutation(np.resize(levels, 8))
        for g in range(8):
            far = levels[np.abs(levels - a[p, g]) >= 10]
            a[p, g + 8] = far[np.random.randint(len(far))]
    return np.exp2(a.ravel()).repeat(32)


BF16 = ml_dtypes.bfloat16


def bf(x):
    return np.asarray(x, np.float32).astype(BF16)


def f64(x):
    return np.asarray(x).astype(np.float64)


B, NB, NL, NG, NK = 256, 1024, 1536, 500, 3
N2 = 2 * NB
L2 = 2 * NL


def relu(v):
    return np.maximum(v, 0.0)


def draw0():
    s, t = mx_kscale(N2), mx_kscale(L2)
    return {'Volt': bf(np.random.standard_normal((B, N2)) * s),
            'IM': bf(np.random.standard_normal((L2, N2)) / np.sqrt(N2) / s[None, :] * t[:, None]),
            'Ybr': bf(np.random.standard_normal((L2, L2)) / np.sqrt(L2) / t[None, :]),
            'L_limit': bf(np.random.random_sample((NL,)) + 0.5),
            'n_o_mu_i_u': bf(np.random.standard_normal((B, NL)))}


def core(Volt, IM, Ybr, L_limit, n_o_mu_i_u):
    d = mxq(f64(Volt), 1, 'e4m3') @ mxq(f64(IM), 1, 'e4m3').T
    Ibr = mxq(d, 1, 'e4m3') @ mxq(f64(Ybr), 1, 'e4m3').T
    m = Ibr[:, :NL] ** 2 + Ibr[:, NL:] ** 2
    g = m - f64(L_limit) ** 2
    mu = f64(n_o_mu_i_u)
    return relu(g).sum(axis=1) + np.abs(mu * g).sum(axis=1) + relu(-mu).sum(axis=1)


def e4m3fn_bytes(y):
    return np.clip(np.asarray(y, np.float64), -448.0, 448.0).astype(np.float32).astype(ml_dtypes.float8_e4m3fn).view(np.uint8)


def e4m3fn_values(b):
    return np.asarray(b, np.uint8).view(ml_dtypes.float8_e4m3fn).astype(np.float64)


def setup_inputs():
    d = draw0()
    x0 = np.asarray(d['Ybr']).astype(np.float64)
    s = (np.max(np.abs(x0), axis=(0,), keepdims=True) / 448.0).astype(np.float32)
    out = {}
    for k, v in d.items():
        if k == 'Ybr':
            out['Ybr_bytes'] = e4m3fn_bytes(x0 / s.astype(np.float64))
            out['Ybr_scale'] = s
        else:
            out[k] = v
    return out


def reference(Volt, IM, Ybr_bytes, Ybr_scale, L_limit, n_o_mu_i_u):
    return core(Volt, IM, e4m3fn_values(Ybr_bytes) * Ybr_scale.astype(np.float64), L_limit, n_o_mu_i_u)

@@ -1,0 +1,344 @@
+from contextlib import ExitStack
+
+import concourse.mybir as mybir
+from concourse.masks import make_identity
+
+F32 = mybir.dt.float32
+BF16 = mybir.dt.bfloat16
+U32 = mybir.dt.uint32
+U8 = mybir.dt.uint8
+FP8 = mybir.dt.float8_e4m3fn
+FP8X4 = mybir.dt.float8_e4m3fn_x4
+ACT = mybir.ActivationFunctionType
+ALU = mybir.AluOpType
+AX = mybir.AxisListType
+
+P = 128
+B, N2, NL = 256, 2048, 1536
+L2 = 2 * NL
+KP = 512
+C1, C2 = N2 // KP, L2 // KP
+ROWS = 256
+RT = 2
+NCH = L2 // ROWS
+NPAIR = NL // ROWS
+GP = 2
+CP = C2 - GP
+KC = CP * KP
+KG = GP * KP
+YB = 9
+TB = 5
+
+FLOPS = 2 * B * L2 * (N2 + L2)
+
+
+def tile_kktloss_pa_kernel(tc, Volt, IM, Ybr_bytes, Ybr_scale, L_limit, n_o_mu_i_u, out):
+    nc = tc.nc
+    with ExitStack() as ctx:
+        keep = ctx.enter_context(tc.tile_pool(name="keep", bufs=1))
+        pool = ctx.enter_context(tc.tile_pool(name="work", bufs=2))
+        psum = ctx.enter_context(tc.psum_pool(name="psum", bufs=1))
+
+        ident = keep.tile([P, P], F32, name="ident")
+        make_identity(nc, ident[:])
+        warm = keep.tile([P, 1], F32, name="warm")
+        nc.vector.memset(warm[:], 0.0)
+        warm2 = keep.tile([P, 1], F32, name="warm2")
+        nc.scalar.activation(out=warm2[:], in_=warm[:], func=ACT.Square)
+
+        scol = keep.tile([P, C2, 4], F32, name="scol")
+        sbc = keep.tile([P, KG], F32, name="sbc")
+        lim = keep.tile([P, NL], BF16, name="lim")
+        lim2 = keep.tile([P, NL], F32, name="lim2")
+        mu = keep.tile([P, RT, NL], BF16, name="mu")
+        mu_neg = keep.tile([P, NL], BF16, name="mu_neg")
+        res = keep.tile([P, P], F32, name="res")
+        sums = keep.tile([P, RT, 2 * NPAIR + 1], F32, name="sums")
+        v_codes = keep.tile([P, C1, B], U32, name="v_codes", align_bytes=64)
+        v_scales = keep.tile([P, C1, B], U8, name="v_scales", align_bytes=64)
+        d_codes = keep.tile([P, C2, B], U32, name="d_codes", align_bytes=64)
+        d_scales = keep.tile([P, C2, B], U8, name="d_scales", align_bytes=64)
+
+        volt_v = Volt.rearrange("(r p) k -> p r k", p=P)
+        im_v = IM.rearrange("(g m t) k -> g m t k", m=P, t=4)
+        y_v = Ybr_bytes.rearrange("(c r p) k -> c p r k", r=RT, p=P)
+
+        raw = {}
+        byts = {}
+        wide = {}
+        prod = {}
+        grouped = {}
+        banks = {}
+        im_q = {}
+        y_q = {}
+        d_bank = {}
+        d_grp = {}
+        y_bank = {}
+
+        def load_im(c):
+            raw[c] = pool.tile([P, RT, N2], BF16, name="raw", bufs=3)
+            src = volt_v if c < 0 else im_v[c // 2][:, 2 * (c % 2):2 * (c % 2) + 2, :]
+            if c < 1:
+                for h in range(2):
+                    nc.sync.dma_start(out=raw[c][:, :, h * 1024:(h + 1) * 1024], in_=src[:, :, h * 1024:(h + 1) * 1024])
+            else:
+                nc.sync.dma_start(out=raw[c][:], in_=src)
+
+        def y_chunk_rows(c):
+            return c // 2 + (c % 2) * NPAIR
+
+        def load_y(c):
+            byts[c] = pool.tile([P, RT, L2], U8, name="ybytes", bufs=3)
+            nc.sync.dma_start(out=byts[c][:], in_=y_v[y_chunk_rows(c)])
+
+        cast_order = [(r, KC, L2) for r in range(RT)] + [(r, h * 1024, (h + 1) * 1024) for h in range(2) for r in range(RT)]
+
+        def cast(c, i):
+            if i == 0:
+                wide[c] = pool.tile([P, RT, L2], BF16, name="wide", bufs=2)
+            r, a, b = cast_order[i]
+            nc.scalar.copy(out=wide[c][:, r, a:b], in_=byts[c][:, r, a:b].bitcast(FP8))
+
+        def scale_g(c, r):
+            if r == 0:
+                prod[c] = pool.tile([P, RT, KG], BF16, name="prod", bufs=2)
+            for g in range(GP):
+                ks = slice(g * KP, (g + 1) * KP)
+                nc.gpsimd.tensor_tensor(out=prod[c][:, r, ks], in0=wide[c][:, r, KC + g * KP:KC + (g + 1) * KP], in1=sbc[:, ks], op=ALU.mult)
+
+        def unit_passes(u):
+            kind, c, h = u
+            if kind == "i":
+                return [2 * h, 2 * h + 1]
+            return [2 * h, 2 * h + 1, CP + h]
+
+        def turn(u):
+            kind, c, h = u
+            banks[u] = []
+            for g in unit_passes(u):
+                bank = psum.tile([P, 2, ROWS], F32, name="turned", bufs=TB)
+                for w in range(2):
+                    for r in range(RT):
+                        if kind == "i":
+                            words = raw[c][:, r, g * KP:(g + 1) * KP].bitcast(F32)
+                        elif g < CP:
+                            words = wide[c][:, r, g * KP:(g + 1) * KP].bitcast(F32)
+                        else:
+                            words = prod[c][:, r, (g - CP) * KP:(g - CP + 1) * KP].bitcast(F32)
+                        nc.tensor.transpose(bank[:, w, r * P:(r + 1) * P], words[:, w::2], ident[:])
+                banks[u].append(bank)
+
+        def empty(u):
+            kind, c, h = u
+            n = len(banks[u])
+            grouped[u] = pool.tile([P, 2, ROWS * 4], BF16, name="grouped", bufs=4, align_bytes=64)
+            if n == 3:
+                grouped[u, 2] = pool.tile([P, ROWS * 4], BF16, name="grouped_g", bufs=3, align_bytes=64)
+            for j, g in enumerate(unit_passes(u)):
+                bank = banks[u][j]
+                dst = grouped[u][:, j, :] if j < 2 else grouped[u, 2][:]
+                if kind == "y" and g < CP:
+                    nc.vector.tensor_tensor(
+                        out=dst.rearrange("p (r w e) -> p r w e", w=2, e=2),
+                        in0=bank[:].rearrange("p w r -> p (w r)").bitcast(BF16).rearrange("p (w r e) -> p r w e", w=2, e=2),
+                        in1=scol[:, g, :].rearrange("p (w e) -> p w e", e=2).unsqueeze(1).to_broadcast([P, ROWS, 2, 2]),
+                        op=ALU.mult)
+                else:
+                    nc.scalar.copy(out=dst.bitcast(F32).rearrange("p (r w) -> p r w", w=2), in_=bank[:].rearrange("p w r -> p r w"))
+
+        def quant(u):
+            kind, c, h = u
+            if kind == "i" and c < 0:
+                cq, sq = v_codes, v_scales
+            elif kind == "i":
+                if h == 0:
+                    im_q[c] = (pool.tile([P, C1, ROWS], U32, name="im_codes", bufs=2, align_bytes=64),
+                               pool.tile([P, C1, ROWS], U8, name="im_scales", bufs=2, align_bytes=64))
+                cq, sq = im_q[c]
+            else:
+                if h == 0:
+                    y_q[c] = (pool.tile([P, C2, ROWS], U32, name="y_codes", bufs=YB, align_bytes=64),
+                              pool.tile([P, C2, ROWS], U8, name="y_scales", bufs=YB, align_bytes=64))
+                cq, sq = y_q[c]
+            nc.vector.quantize_mx(
+                out=cq[:, 2 * h:2 * h + 2, :].rearrange("p g r -> p (g r)").bitcast(FP8X4),
+                scales=sq[:, 2 * h:2 * h + 2, :].rearrange("p g r -> p (g r)"),
+                in_=grouped[u][:].rearrange("p g k -> p (g k)"))
+            if kind == "y":
+                nc.vector.quantize_mx(out=cq[:, CP + h, :].bitcast(FP8X4), scales=sq[:, CP + h, :], in_=grouped[u, 2][:])
+
+        def mx1(c):
+            gp, odd = c // 2, c % 2
+            if odd == 0:
+                d_bank[gp] = [psum.tile([P, 4, P], F32, name="acc", bufs=8 - TB) for hb in range(2)]
+            cq, sq = im_q[c]
+            for hb in range(2):
+                bs = slice(hb * P, (hb + 1) * P)
+                for r in range(RT):
+                    rs = slice(r * P, (r + 1) * P)
+                    for g in range(C1):
+                        nc.tensor.matmul_mx(
+                            out=d_bank[gp][hb][:, 2 * odd + r, :],
+                            lhsT=cq[:, g, rs].bitcast(FP8X4), lhsT_scale=sq[:, g, rs],
+                            rhs=v_codes[:, g, bs].bitcast(FP8X4), rhs_scale=v_scales[:, g, bs],
+                            start=(g == 0), stop=(g == C1 - 1))
+
+        def empty_d(gp):
+            d_grp[gp] = pool.tile([P, B, 4], BF16, name="d_grouped", bufs=2, align_bytes=64)
+            for hb in range(2):
+                nc.scalar.copy(out=d_grp[gp][:, hb * P:(hb + 1) * P, :], in_=d_bank[gp][hb][:].rearrange("p t b -> p b t"))
+
+        def quant_d(gp):
+            nc.vector.quantize_mx(out=d_codes[:, gp, :].bitcast(FP8X4), scales=d_scales[:, gp, :], in_=d_grp[gp][:].rearrange("p b t -> p (b t)"))
+
+        def mx2(c, m):
+            if m == 0:
+                y_bank[c] = psum.tile([P, RT, ROWS], F32, name="acc", bufs=8 - TB)
+            cq, sq = y_q[c]
+            ms = slice(m * P, (m + 1) * P)
+            for g in range(C2):
+                nc.tensor.matmul_mx(
+                    out=y_bank[c][:, m, :],
+                    lhsT=d_codes[:, g, ms].bitcast(FP8X4), lhsT_scale=d_scales[:, g, ms],
+                    rhs=cq[:, g, :].bitcast(FP8X4), rhs_scale=sq[:, g, :],
+                    start=(g == 0), stop=(g == C2 - 1))
+
+        sq_t = {}
+        w_t = {}
+        g_t = {}
+        u_t = {}
+
+        def square(c, m=None):
+            if m is None or m == 0:
+                sq_t[c] = pool.tile([P, RT, ROWS], F32, name="sq_im" if c % 2 else "sq_re", bufs=2)
+            sl = slice(None) if m is None else slice(m, m + 1)
+            nc.scalar.activation(out=sq_t[c][:, sl, :], in_=y_bank[c][:, sl, :], func=ACT.Square)
+
+        def less_limit(i):
+            ls = slice(i * ROWS, (i + 1) * ROWS)
+            w_t[i] = pool.tile([P, RT, ROWS], F32, name="w_t", bufs=2)
+            nc.vector.tensor_tensor(out=w_t[i][:], in0=sq_t[2 * i][:], in1=lim2[:, ls].unsqueeze(1).to_broadcast([P, RT, ROWS]), op=ALU.subtract)
+
+        def combine(i, m=None):
+            ls = slice(i * ROWS, (i + 1) * ROWS)
+            if m is None or m == 0:
+                g_t[i] = pool.tile([P, RT, ROWS], F32, name="g_t", bufs=2)
+                u_t[i] = pool.tile([P, RT, ROWS], F32, name="u_t", bufs=2)
+            sl = slice(None) if m is None else slice(m, m + 1)
+            nc.vector.tensor_tensor(out=g_t[i][:, sl, :], in0=w_t[i][:, sl, :], in1=sq_t[2 * i + 1][:, sl, :], op=ALU.add)
+            nc.vector.tensor_tensor(out=u_t[i][:, sl, :], in0=g_t[i][:, sl, :], in1=mu[:, sl, ls], op=ALU.mult)
+
+        def total(i, m):
+            nc.scalar.activation(out=g_t[i][:, m, :], in_=g_t[i][:, m, :], func=ACT.Relu, accum_out=sums[:, m, 2 * i:2 * i + 1])
+            nc.scalar.activation(out=u_t[i][:, m, :], in_=u_t[i][:, m, :], func=ACT.Abs, accum_out=sums[:, m, 2 * i + 1:2 * i + 2])
+
+        def mu_total(m):
+            nc.scalar.activation(out=mu_neg[:], in_=mu[:, m, :], func=ACT.Relu, scale=-1.0, accum_out=sums[:, m, 2 * NPAIR:2 * NPAIR + 1])
+
+        im_u = [("i", c, h) for c in range(NCH) for h in range(2)]
+        y_u = [("y", c, h) for c in range(NCH) for h in range(2)]
+        seq = [("i", -1, 0), ("i", -1, 1)]
+        for k in range(8):
+            a = im_u[3 * k:3 * k + 3]
+            b = y_u[2 * k:2 * k + 2]
+            seq += [a[0], b[0], a[1], b[1], a[2]]
+        seq += y_u[16:]
+        n = len(seq)
+        pos = {u: s for s, u in enumerate(seq)}
+
+        qstep = {}
+        for s, u in enumerate(seq):
+            t = s + 1
+            while t < n and seq[t][0] != "y":
+                t += 1
+            qstep[u] = t
+
+        pe_jobs = {}
+        s_jobs = {}
+        v_jobs = {}
+        casts = {}
+
+        def at(table, step, fn, *args):
+            table.setdefault(step, []).append((fn, args))
+
+        first_y = {c: pos["y", c, 0] for c in range(NCH)}
+        for c in range(NCH):
+            a = first_y[c - 1] if c else 0
+            b = first_y[c] if c else 0
+            for i in range(6):
+                st = a + (b - a) * i // 6
+                at(casts, st, cast, c, i)
+                if i < 2:
+                    at(casts, st, scale_g, c, i)
+        t = 0
+        for c in range(NCH):
+            t = qstep["i", c, 1] + 1
+            at(pe_jobs, t, mx1, c)
+            if c % 2:
+                at(s_jobs, t, empty_d, c // 2)
+                at(v_jobs, t + 1, quant_d, c // 2)
+        step = t + 3
+        for c in range(NCH):
+            ready = max(step, qstep["y", c, 1] + 1)
+            at(pe_jobs, ready, mx2, c, 0)
+            at(pe_jobs, ready, mx2, c, 1)
+            if c == NCH - 1:
+                for m in range(RT):
+                    at(s_jobs, ready, square, c, m)
+                    at(v_jobs, ready, combine, c // 2, m)
+                    at(s_jobs, ready + 1, total, c // 2, m)
+            else:
+                at(s_jobs, ready, square, c)
+                if c % 2 == 0:
+                    at(v_jobs, ready + 1, less_limit, c // 2)
+                else:
+                    at(v_jobs, ready + 1, combine, c // 2)
+                    at(s_jobs, ready + 2, total, c // 2, 0)
+                    at(s_jobs, ready + 2, total, c // 2, 1)
+            step = ready + 1
+        end = max(max(pe_jobs), max(s_jobs), max(v_jobs)) + 1
+
+        def do(table, s):
+            for fn, args in table.get(s, []):
+                fn(*args)
+
+        with tc.manual_schedule():
+            load_im(-1)
+            load_y(0)
+            load_im(0)
+            load_im(1)
+            load_y(1)
+            nc.scalar.dma_start(out=sbc[:], in_=Ybr_scale[:, KC:L2].rearrange("o k -> (o k)").partition_broadcast(P))
+            nc.scalar.dma_start(out=scol[:], in_=Ybr_scale.rearrange("o (g p t) -> p (o g) t", p=P, t=4))
+            nc.gpsimd.memset(res[:], 0.0)
+            for s in range(max(n, end)):
+                if s < n:
+                    kind, c, h = seq[s]
+                    if kind == "i" and h == 0 and c + 2 < NCH and c >= 0:
+                        load_im(c + 2)
+                    if kind == "y" and h == 0 and c + 2 < NCH:
+                        load_y(c + 2)
+                    turn(seq[s])
+                do(pe_jobs, s)
+                if s < n:
+                    do(casts, s)
+                    empty(seq[s])
+                for u in seq:
+                    if qstep[u] == s:
+                        quant(u)
+                do(s_jobs, s)
+                do(v_jobs, s)
+                if s == 12:
+                    nc.scalar.dma_start(out=lim[:], in_=L_limit.partition_broadcast(P))
+                    nc.scalar.dma_start(out=mu[:], in_=n_o_mu_i_u.rearrange("(r p) l -> p r l", p=P))
+                if s == 20:
+                    nc.gpsimd.tensor_tensor(out=lim2[:], in0=lim[:], in1=lim[:], op=ALU.mult)
+                if s in (24, 30):
+                    mu_total(s // 30)
+
+            nc.vector.tensor_reduce(out=res[:, 0:RT], in_=sums[:], axis=AX.X, op=ALU.add)
+            fin = psum.tile([P, P], F32, name="acc", bufs=8 - TB)
+            nc.tensor.transpose(fin[:], res[:], ident[:])
+            fin_sb = keep.tile([P, P], F32, name="fin_sb")
+            nc.vector.tensor_copy(out=fin_sb[:], in_=fin[:])
+            nc.sync.dma_start(out=out.rearrange("(m p) -> m p", p=P), in_=fin_sb[0:RT, :])

@@ -22,12 +22,17 @@ ROWS = 256
 RT = 2
 NCH = L2 // ROWS
 NPAIR = NL // ROWS
-GP = 2
-CP = C2 - GP
-KC = CP * KP
-KG = GP * KP
+UP = 3
+KU = UP * KP
 YB = 9
+YN = 14
 TB = 5
+IB = 2
+WB = 3
+GB = 4
+LEAD = 3
+LAG = 2
+PER = 2
 
 FLOPS = 2 * B * L2 * (N2 + L2)
 
@@ -46,8 +51,7 @@ def tile_kktloss_pa_kernel(tc, Volt, IM, Ybr_bytes, Ybr_scale, L_limit, n_o_mu_i
         warm2 = keep.tile([P, 1], F32, name="warm2")
         nc.scalar.activation(out=warm2[:], in_=warm[:], func=ACT.Square)
 
-        scol = keep.tile([P, C2, 4], F32, name="scol")
-        sbc = keep.tile([P, KG], F32, name="sbc")
+        sbc = keep.tile([P, L2], F32, name="sbc")
         lim = keep.tile([P, NL], BF16, name="lim")
         lim2 = keep.tile([P, NL], F32, name="lim2")
         mu = keep.tile([P, RT, NL], BF16, name="mu")
@@ -91,81 +95,52 @@ def tile_kktloss_pa_kernel(tc, Volt, IM, Ybr_bytes, Ybr_scale, L_limit, n_o_mu_i
             byts[c] = pool.tile([P, RT, L2], U8, name="ybytes", bufs=3)
             nc.sync.dma_start(out=byts[c][:], in_=y_v[y_chunk_rows(c)])
 
-        cast_order = [(r, KC, L2) for r in range(RT)] + [(r, h * 1024, (h + 1) * 1024) for h in range(2) for r in range(RT)]
-
-        def cast(c, i):
-            if i == 0:
-                wide[c] = pool.tile([P, RT, L2], BF16, name="wide", bufs=2)
-            r, a, b = cast_order[i]
-            nc.scalar.copy(out=wide[c][:, r, a:b], in_=byts[c][:, r, a:b].bitcast(FP8))
-
-        def scale_g(c, r):
+        def product(c, h, r):
             if r == 0:
-                prod[c] = pool.tile([P, RT, KG], BF16, name="prod", bufs=2)
-            for g in range(GP):
-                ks = slice(g * KP, (g + 1) * KP)
-                nc.gpsimd.tensor_tensor(out=prod[c][:, r, ks], in0=wide[c][:, r, KC + g * KP:KC + (g + 1) * KP], in1=sbc[:, ks], op=ALU.mult)
-
-        def unit_passes(u):
-            kind, c, h = u
-            if kind == "i":
-                return [2 * h, 2 * h + 1]
-            return [2 * h, 2 * h + 1, CP + h]
+                wide[c, h] = pool.tile([P, RT, KU], BF16, name="wide", bufs=WB)
+            ks = slice(h * KU, (h + 1) * KU)
+            nc.vector.tensor_tensor(out=wide[c, h][:, r, :], in0=byts[c][:, r, ks].bitcast(FP8), in1=sbc[:, ks], op=ALU.mult)
 
         def turn(u):
             kind, c, h = u
             banks[u] = []
-            for g in unit_passes(u):
+            for j in range(2 if kind == "i" else UP):
                 bank = psum.tile([P, 2, ROWS], F32, name="turned", bufs=TB)
                 for w in range(2):
                     for r in range(RT):
                         if kind == "i":
-                            words = raw[c][:, r, g * KP:(g + 1) * KP].bitcast(F32)
-                        elif g < CP:
-                            words = wide[c][:, r, g * KP:(g + 1) * KP].bitcast(F32)
+                            words = raw[c][:, r, (2 * h + j) * KP:(2 * h + j + 1) * KP].bitcast(F32)
                         else:
-                            words = prod[c][:, r, (g - CP) * KP:(g - CP + 1) * KP].bitcast(F32)
+                            words = wide[c, h][:, r, j * KP:(j + 1) * KP].bitcast(F32)
                         nc.tensor.transpose(bank[:, w, r * P:(r + 1) * P], words[:, w::2], ident[:])
                 banks[u].append(bank)
 
         def empty(u):
-            kind, c, h = u
             n = len(banks[u])
-            grouped[u] = pool.tile([P, 2, ROWS * 4], BF16, name="grouped", bufs=4, align_bytes=64)
-            if n == 3:
-                grouped[u, 2] = pool.tile([P, ROWS * 4], BF16, name="grouped_g", bufs=3, align_bytes=64)
-            for j, g in enumerate(unit_passes(u)):
-                bank = banks[u][j]
-                dst = grouped[u][:, j, :] if j < 2 else grouped[u, 2][:]
-                if kind == "y" and g < CP:
-                    nc.vector.tensor_tensor(
-                        out=dst.rearrange("p (r w e) -> p r w e", w=2, e=2),
-                        in0=bank[:].rearrange("p w r -> p (w r)").bitcast(BF16).rearrange("p (w r e) -> p r w e", w=2, e=2),
-                        in1=scol[:, g, :].rearrange("p (w e) -> p w e", e=2).unsqueeze(1).to_broadcast([P, ROWS, 2, 2]),
-                        op=ALU.mult)
-                else:
-                    nc.scalar.copy(out=dst.bitcast(F32).rearrange("p (r w) -> p r w", w=2), in_=bank[:].rearrange("p w r -> p r w"))
+            grouped[u] = pool.tile([P, UP, ROWS * 4], BF16, name="grouped", bufs=GB, align_bytes=64)
+            for j in range(n):
+                nc.scalar.copy(out=grouped[u][:, j, :].bitcast(F32).rearrange("p (r w) -> p r w", w=2), in_=banks[u][j][:].rearrange("p w r -> p r w"))
 
         def quant(u):
             kind, c, h = u
+            n = len(banks[u])
             if kind == "i" and c < 0:
                 cq, sq = v_codes, v_scales
             elif kind == "i":
                 if h == 0:
-                    im_q[c] = (pool.tile([P, C1, ROWS], U32, name="im_codes", bufs=2, align_bytes=64),
-                               pool.tile([P, C1, ROWS], U8, name="im_scales", bufs=2, align_bytes=64))
+                    im_q[c] = (pool.tile([P, C1, ROWS], U32, name="im_codes", bufs=IB, align_bytes=64),
+                               pool.tile([P, C1, ROWS], U8, name="im_scales", bufs=IB, align_bytes=64))
                 cq, sq = im_q[c]
             else:
                 if h == 0:
                     y_q[c] = (pool.tile([P, C2, ROWS], U32, name="y_codes", bufs=YB, align_bytes=64),
                               pool.tile([P, C2, ROWS], U8, name="y_scales", bufs=YB, align_bytes=64))
                 cq, sq = y_q[c]
-            nc.vector.quantize_mx(
-                out=cq[:, 2 * h:2 * h + 2, :].rearrange("p g r -> p (g r)").bitcast(FP8X4),
-                scales=sq[:, 2 * h:2 * h + 2, :].rearrange("p g r -> p (g r)"),
-                in_=grouped[u][:].rearrange("p g k -> p (g k)"))
-            if kind == "y":
-                nc.vector.quantize_mx(out=cq[:, CP + h, :].bitcast(FP8X4), scales=sq[:, CP + h, :], in_=grouped[u, 2][:])
+            for a, b in ((0, 2), (2, 3))[:n - 1]:
+                nc.vector.quantize_mx(
+                    out=cq[:, n * h + a:n * h + b, :].rearrange("p g r -> p (g r)").bitcast(FP8X4),
+                    scales=sq[:, n * h + a:n * h + b, :].rearrange("p g r -> p (g r)"),
+                    in_=grouped[u][:, a:b, :].rearrange("p g k -> p (g k)"))
 
         def mx1(c):
             gp, odd = c // 2, c % 2
@@ -238,38 +213,29 @@ def tile_kktloss_pa_kernel(tc, Volt, IM, Ybr_bytes, Ybr_scale, L_limit, n_o_mu_i
         im_u = [("i", c, h) for c in range(NCH) for h in range(2)]
         y_u = [("y", c, h) for c in range(NCH) for h in range(2)]
         seq = [("i", -1, 0), ("i", -1, 1)]
-        for k in range(8):
-            a = im_u[3 * k:3 * k + 3]
-            b = y_u[2 * k:2 * k + 2]
-            seq += [a[0], b[0], a[1], b[1], a[2]]
-        seq += y_u[16:]
+        ny = 0
+        for k, u in enumerate(im_u):
+            seq.append(u)
+            if (k + 1) * YN // 24 > ny:
+                seq.append(y_u[ny])
+                ny += 1
+        seq += y_u[ny:]
         n = len(seq)
         pos = {u: s for s, u in enumerate(seq)}
-
-        qstep = {}
-        for s, u in enumerate(seq):
-            t = s + 1
-            while t < n and seq[t][0] != "y":
-                t += 1
-            qstep[u] = t
 
         pe_jobs = {}
         s_jobs = {}
         v_jobs = {}
-        casts = {}
+        prods = {}
 
         def at(table, step, fn, *args):
             table.setdefault(step, []).append((fn, args))
 
-        first_y = {c: pos["y", c, 0] for c in range(NCH)}
+        qstep = {u: s + LAG for s, u in enumerate(seq)}
         for c in range(NCH):
-            a = first_y[c - 1] if c else 0
-            b = first_y[c] if c else 0
-            for i in range(6):
-                st = a + (b - a) * i // 6
-                at(casts, st, cast, c, i)
-                if i < 2:
-                    at(casts, st, scale_g, c, i)
+            for h in range(2):
+                for r in range(RT):
+                    at(prods, pos["y", c, h] - LEAD + r, product, c, h, r)
         t = 0
         for c in range(NCH):
             t = qstep["i", c, 1] + 1
@@ -277,7 +243,8 @@ def tile_kktloss_pa_kernel(tc, Volt, IM, Ybr_bytes, Ybr_scale, L_limit, n_o_mu_i
             if c % 2:
                 at(s_jobs, t, empty_d, c // 2)
                 at(v_jobs, t + 1, quant_d, c // 2)
-        step = t + 3
+        step = t + 2
+        used = 0
         for c in range(NCH):
             ready = max(step, qstep["y", c, 1] + 1)
             at(pe_jobs, ready, mx2, c, 0)
@@ -295,7 +262,9 @@ def tile_kktloss_pa_kernel(tc, Volt, IM, Ybr_bytes, Ybr_scale, L_limit, n_o_mu_i
                     at(v_jobs, ready + 1, combine, c // 2)
                     at(s_jobs, ready + 2, total, c // 2, 0)
                     at(s_jobs, ready + 2, total, c // 2, 1)
-            step = ready + 1
+            used = used + 1 if ready == step else 1
+            step = ready + (used == PER)
+            used = 0 if used == PER else used
         end = max(max(pe_jobs), max(s_jobs), max(v_jobs)) + 1
 
         def do(table, s):
@@ -303,30 +272,29 @@ def tile_kktloss_pa_kernel(tc, Volt, IM, Ybr_bytes, Ybr_scale, L_limit, n_o_mu_i
                 fn(*args)
 
         with tc.manual_schedule():
-            load_im(-1)
-            load_y(0)
-            load_im(0)
-            load_im(1)
-            load_y(1)
-            nc.scalar.dma_start(out=sbc[:], in_=Ybr_scale[:, KC:L2].rearrange("o k -> (o k)").partition_broadcast(P))
-            nc.scalar.dma_start(out=scol[:], in_=Ybr_scale.rearrange("o (g p t) -> p (o g) t", p=P, t=4))
             nc.gpsimd.memset(res[:], 0.0)
-            for s in range(max(n, end)):
-                if s < n:
+            for h in range(2):
+                nc.scalar.dma_start(out=sbc[:, h * KU:(h + 1) * KU], in_=Ybr_scale[:, h * KU:(h + 1) * KU].rearrange("o k -> (o k)").partition_broadcast(P))
+            load_y(0)
+            load_im(-1)
+            load_im(0)
+            load_y(1)
+            load_im(1)
+            for s in range(-LEAD, max(n, end)):
+                if 0 <= s < n:
                     kind, c, h = seq[s]
-                    if kind == "i" and h == 0 and c + 2 < NCH and c >= 0:
+                    if kind == "i" and h == 0 and 0 <= c < NCH - 2:
                         load_im(c + 2)
                     if kind == "y" and h == 0 and c + 2 < NCH:
                         load_y(c + 2)
                     turn(seq[s])
                 do(pe_jobs, s)
-                if s < n:
-                    do(casts, s)
+                if 0 <= s < n:
                     empty(seq[s])
-                for u in seq:
-                    if qstep[u] == s:
-                        quant(u)
                 do(s_jobs, s)
+                do(prods, s)
+                if 0 <= s - LAG < n:
+                    quant(seq[s - LAG])
                 do(v_jobs, s)
                 if s == 12:
                     nc.scalar.dma_start(out=lim[:], in_=L_limit.partition_broadcast(P))

@@ -24,15 +24,21 @@ NCH = L2 // ROWS
 NPAIR = NL // ROWS
 UP = 3
 KU = UP * KP
-YB = 9
+YB = 8
 YN = 14
 TB = 5
 IB = 2
-WB = 3
-GB = 4
 LEAD = 3
 LAG = 2
 PER = 2
+NA = 12
+MODE = "CCG"
+GEPI = 0
+RAWB = 3
+GIB = 2
+GYB = 2
+WB = 3
+YBB = 3
 
 FLOPS = 2 * B * L2 * (N2 + L2)
 
@@ -51,11 +57,11 @@ def tile_kktloss_pa_kernel(tc, Volt, IM, Ybr_bytes, Ybr_scale, L_limit, n_o_mu_i
         warm2 = keep.tile([P, 1], F32, name="warm2")
         nc.scalar.activation(out=warm2[:], in_=warm[:], func=ACT.Square)
 
+        scol = keep.tile([P, C2, 4], F32, name="scol")
         sbc = keep.tile([P, L2], F32, name="sbc")
         lim = keep.tile([P, NL], BF16, name="lim")
         lim2 = keep.tile([P, NL], F32, name="lim2")
         mu = keep.tile([P, RT, NL], BF16, name="mu")
-        mu_neg = keep.tile([P, NL], BF16, name="mu_neg")
         res = keep.tile([P, P], F32, name="res")
         sums = keep.tile([P, RT, 2 * NPAIR + 1], F32, name="sums")
         v_codes = keep.tile([P, C1, B], U32, name="v_codes", align_bytes=64)
@@ -67,20 +73,11 @@ def tile_kktloss_pa_kernel(tc, Volt, IM, Ybr_bytes, Ybr_scale, L_limit, n_o_mu_i
         im_v = IM.rearrange("(g m t) k -> g m t k", m=P, t=4)
         y_v = Ybr_bytes.rearrange("(c r p) k -> c p r k", r=RT, p=P)
 
-        raw = {}
-        byts = {}
-        wide = {}
-        prod = {}
-        grouped = {}
-        banks = {}
-        im_q = {}
-        y_q = {}
-        d_bank = {}
-        d_grp = {}
-        y_bank = {}
+        raw, byts, wide, prod, grouped, banks, im_q, y_q = {}, {}, {}, {}, {}, {}, {}, {}
+        d_bank, d_grp, y_bank = {}, {}, {}
 
         def load_im(c):
-            raw[c] = pool.tile([P, RT, N2], BF16, name="raw", bufs=3)
+            raw[c] = pool.tile([P, RT, N2], BF16, name="raw", bufs=RAWB)
             src = volt_v if c < 0 else im_v[c // 2][:, 2 * (c % 2):2 * (c % 2) + 2, :]
             if c < 1:
                 for h in range(2):
@@ -92,55 +89,102 @@ def tile_kktloss_pa_kernel(tc, Volt, IM, Ybr_bytes, Ybr_scale, L_limit, n_o_mu_i
             return c // 2 + (c % 2) * NPAIR
 
         def load_y(c):
-            byts[c] = pool.tile([P, RT, L2], U8, name="ybytes", bufs=3)
-            nc.sync.dma_start(out=byts[c][:], in_=y_v[y_chunk_rows(c)])
+            byts[c] = pool.tile([P, RT, L2], U8, name="ybytes", bufs=YBB)
+            cuts = (0, KU, L2) if c == 0 else (0, L2)
+            for a, b in zip(cuts, cuts[1:]):
+                nc.sync.dma_start(out=byts[c][:, :, a:b], in_=y_v[y_chunk_rows(c)][:, :, a:b])
 
-        def product(c, h, r):
+        def spread(g):
+            bank = psum.tile([P, 4, P], F32, name="turned", bufs=TB)
+            for t in range(4):
+                nc.tensor.transpose(bank[:, t, :], scol[:, g, t:t + 1].to_broadcast([P, P]), ident[:])
+            dst = sbc[:, g * KP:(g + 1) * KP].rearrange("p (n t) -> p n t", t=4)
+            src = bank[:].rearrange("p t n -> p n t")
+            if g in (0, 2):
+                nc.vector.tensor_copy(out=dst, in_=src)
+            else:
+                nc.scalar.copy(out=dst, in_=src)
+
+        def mode(u):
+            kind, c, h = u
+            if kind == "i":
+                return "A" * 2
+            return "A" * UP if c < NA else MODE
+
+        def new_wide(c, h):
+            wide[c, h] = pool.tile([P, RT, KU], BF16, name="wide", bufs=WB)
+
+        def widen(c, h, r):
             if r == 0:
-                wide[c, h] = pool.tile([P, RT, KU], BF16, name="wide", bufs=WB)
+                new_wide(c, h)
             ks = slice(h * KU, (h + 1) * KU)
-            nc.vector.tensor_tensor(out=wide[c, h][:, r, :], in0=byts[c][:, r, ks].bitcast(FP8), in1=sbc[:, ks], op=ALU.mult)
+            src = byts[c][:, r, ks].bitcast(FP8)
+            if c < NA:
+                nc.vector.tensor_tensor(out=wide[c, h][:, r, :], in0=src, in1=sbc[:, ks], op=ALU.mult)
+            else:
+                nc.scalar.copy(out=wide[c, h][:, r, :], in_=src)
+
+        def scale_g(c, h, r):
+            if r == 0:
+                prod[c, h] = pool.tile([P, RT, KP], BF16, name="prod", bufs=2)
+            j = MODE.index("G")
+            ks = slice(h * KU + j * KP, h * KU + (j + 1) * KP)
+            nc.gpsimd.tensor_tensor(out=prod[c, h][:, r, :], in0=wide[c, h][:, r, j * KP:(j + 1) * KP], in1=sbc[:, ks], op=ALU.mult)
 
         def turn(u):
             kind, c, h = u
             banks[u] = []
-            for j in range(2 if kind == "i" else UP):
+            for j, md in enumerate(mode(u)):
                 bank = psum.tile([P, 2, ROWS], F32, name="turned", bufs=TB)
                 for w in range(2):
                     for r in range(RT):
                         if kind == "i":
                             words = raw[c][:, r, (2 * h + j) * KP:(2 * h + j + 1) * KP].bitcast(F32)
+                        elif md == "G":
+                            words = prod[c, h][:, r, :].bitcast(F32)
                         else:
                             words = wide[c, h][:, r, j * KP:(j + 1) * KP].bitcast(F32)
                         nc.tensor.transpose(bank[:, w, r * P:(r + 1) * P], words[:, w::2], ident[:])
                 banks[u].append(bank)
 
         def empty(u):
-            n = len(banks[u])
-            grouped[u] = pool.tile([P, UP, ROWS * 4], BF16, name="grouped", bufs=GB, align_bytes=64)
-            for j in range(n):
-                nc.scalar.copy(out=grouped[u][:, j, :].bitcast(F32).rearrange("p (r w) -> p r w", w=2), in_=banks[u][j][:].rearrange("p w r -> p r w"))
-
-        def quant(u):
             kind, c, h = u
             n = len(banks[u])
+            if h == 0:
+                if kind == "i":
+                    grouped[kind, c] = pool.tile([P, C1, ROWS * 4], BF16, name="grouped_i", bufs=GIB, align_bytes=64)
+                else:
+                    grouped[kind, c] = pool.tile([P, C2, ROWS * 4], BF16, name="grouped_y", bufs=GYB, align_bytes=64)
+            for j, md in enumerate(mode(u)):
+                g = n * h + j
+                dst = grouped[kind, c][:, g, :]
+                bank = banks[u][j]
+                if md == "C":
+                    nc.vector.tensor_tensor(
+                        out=dst.rearrange("p (r w e) -> p r w e", w=2, e=2),
+                        in0=bank[:].rearrange("p w r -> p (w r)").bitcast(BF16).rearrange("p (w r e) -> p r w e", w=2, e=2),
+                        in1=scol[:, g, :].rearrange("p (w e) -> p w e", e=2).unsqueeze(1).to_broadcast([P, ROWS, 2, 2]),
+                        op=ALU.mult)
+                else:
+                    nc.scalar.copy(out=dst.bitcast(F32).rearrange("p (r w) -> p r w", w=2), in_=bank[:].rearrange("p w r -> p r w"))
+
+        def quant(kind, c, a, b):
             if kind == "i" and c < 0:
                 cq, sq = v_codes, v_scales
             elif kind == "i":
-                if h == 0:
+                if a == 0:
                     im_q[c] = (pool.tile([P, C1, ROWS], U32, name="im_codes", bufs=IB, align_bytes=64),
                                pool.tile([P, C1, ROWS], U8, name="im_scales", bufs=IB, align_bytes=64))
                 cq, sq = im_q[c]
             else:
-                if h == 0:
+                if a == 0:
                     y_q[c] = (pool.tile([P, C2, ROWS], U32, name="y_codes", bufs=YB, align_bytes=64),
                               pool.tile([P, C2, ROWS], U8, name="y_scales", bufs=YB, align_bytes=64))
                 cq, sq = y_q[c]
-            for a, b in ((0, 2), (2, 3))[:n - 1]:
-                nc.vector.quantize_mx(
-                    out=cq[:, n * h + a:n * h + b, :].rearrange("p g r -> p (g r)").bitcast(FP8X4),
-                    scales=sq[:, n * h + a:n * h + b, :].rearrange("p g r -> p (g r)"),
-                    in_=grouped[u][:, a:b, :].rearrange("p g k -> p (g k)"))
+            nc.vector.quantize_mx(
+                out=cq[:, a:b, :].rearrange("p g r -> p (g r)").bitcast(FP8X4),
+                scales=sq[:, a:b, :].rearrange("p g r -> p (g r)"),
+                in_=grouped[kind, c][:, a:b, :].rearrange("p g k -> p (g k)"))
 
         def mx1(c):
             gp, odd = c // 2, c % 2
@@ -166,22 +210,19 @@ def tile_kktloss_pa_kernel(tc, Volt, IM, Ybr_bytes, Ybr_scale, L_limit, n_o_mu_i
         def quant_d(gp):
             nc.vector.quantize_mx(out=d_codes[:, gp, :].bitcast(FP8X4), scales=d_scales[:, gp, :], in_=d_grp[gp][:].rearrange("p b t -> p (b t)"))
 
-        def mx2(c, m):
-            if m == 0:
+        def mx2(c, m, ga=0, gb=C2):
+            if m == 0 and ga == 0:
                 y_bank[c] = psum.tile([P, RT, ROWS], F32, name="acc", bufs=8 - TB)
             cq, sq = y_q[c]
             ms = slice(m * P, (m + 1) * P)
-            for g in range(C2):
+            for g in range(ga, gb):
                 nc.tensor.matmul_mx(
                     out=y_bank[c][:, m, :],
                     lhsT=d_codes[:, g, ms].bitcast(FP8X4), lhsT_scale=d_scales[:, g, ms],
                     rhs=cq[:, g, :].bitcast(FP8X4), rhs_scale=sq[:, g, :],
                     start=(g == 0), stop=(g == C2 - 1))
 
-        sq_t = {}
-        w_t = {}
-        g_t = {}
-        u_t = {}
+        sq_t, u_t = {}, {}
 
         def square(c, m=None):
             if m is None or m == 0:
@@ -189,26 +230,27 @@ def tile_kktloss_pa_kernel(tc, Volt, IM, Ybr_bytes, Ybr_scale, L_limit, n_o_mu_i
             sl = slice(None) if m is None else slice(m, m + 1)
             nc.scalar.activation(out=sq_t[c][:, sl, :], in_=y_bank[c][:, sl, :], func=ACT.Square)
 
+        def two_input(i):
+            return nc.gpsimd if i < GEPI else nc.vector
+
         def less_limit(i):
             ls = slice(i * ROWS, (i + 1) * ROWS)
-            w_t[i] = pool.tile([P, RT, ROWS], F32, name="w_t", bufs=2)
-            nc.vector.tensor_tensor(out=w_t[i][:], in0=sq_t[2 * i][:], in1=lim2[:, ls].unsqueeze(1).to_broadcast([P, RT, ROWS]), op=ALU.subtract)
+            two_input(i).tensor_tensor(out=sq_t[2 * i][:], in0=sq_t[2 * i][:], in1=lim2[:, ls].unsqueeze(1).to_broadcast([P, RT, ROWS]), op=ALU.subtract)
 
         def combine(i, m=None):
             ls = slice(i * ROWS, (i + 1) * ROWS)
             if m is None or m == 0:
-                g_t[i] = pool.tile([P, RT, ROWS], F32, name="g_t", bufs=2)
                 u_t[i] = pool.tile([P, RT, ROWS], F32, name="u_t", bufs=2)
             sl = slice(None) if m is None else slice(m, m + 1)
-            nc.vector.tensor_tensor(out=g_t[i][:, sl, :], in0=w_t[i][:, sl, :], in1=sq_t[2 * i + 1][:, sl, :], op=ALU.add)
-            nc.vector.tensor_tensor(out=u_t[i][:, sl, :], in0=g_t[i][:, sl, :], in1=mu[:, sl, ls], op=ALU.mult)
+            two_input(i).tensor_tensor(out=sq_t[2 * i][:, sl, :], in0=sq_t[2 * i][:, sl, :], in1=sq_t[2 * i + 1][:, sl, :], op=ALU.add)
+            two_input(i).tensor_tensor(out=u_t[i][:, sl, :], in0=sq_t[2 * i][:, sl, :], in1=mu[:, sl, ls], op=ALU.mult)
 
         def total(i, m):
-            nc.scalar.activation(out=g_t[i][:, m, :], in_=g_t[i][:, m, :], func=ACT.Relu, accum_out=sums[:, m, 2 * i:2 * i + 1])
+            nc.scalar.activation(out=sq_t[2 * i][:, m, :], in_=sq_t[2 * i][:, m, :], func=ACT.Relu, accum_out=sums[:, m, 2 * i:2 * i + 1])
             nc.scalar.activation(out=u_t[i][:, m, :], in_=u_t[i][:, m, :], func=ACT.Abs, accum_out=sums[:, m, 2 * i + 1:2 * i + 2])
 
         def mu_total(m):
-            nc.scalar.activation(out=mu_neg[:], in_=mu[:, m, :], func=ACT.Relu, scale=-1.0, accum_out=sums[:, m, 2 * NPAIR:2 * NPAIR + 1])
+            nc.scalar.activation(out=lim[:], in_=mu[:, m, :], func=ACT.Relu, scale=-1.0, accum_out=sums[:, m, 2 * NPAIR:2 * NPAIR + 1])
 
         im_u = [("i", c, h) for c in range(NCH) for h in range(2)]
         y_u = [("y", c, h) for c in range(NCH) for h in range(2)]
@@ -223,22 +265,39 @@ def tile_kktloss_pa_kernel(tc, Volt, IM, Ybr_bytes, Ybr_scale, L_limit, n_o_mu_i
         n = len(seq)
         pos = {u: s for s, u in enumerate(seq)}
 
-        pe_jobs = {}
-        s_jobs = {}
-        v_jobs = {}
-        prods = {}
+        pe_jobs, s_jobs, v_jobs, g_jobs, w_jobs = {}, {}, {}, {}, {}
 
         def at(table, step, fn, *args):
             table.setdefault(step, []).append((fn, args))
 
-        qstep = {u: s + LAG for s, u in enumerate(seq)}
+        done = {}
+        for c in range(-1, NCH):
+            if c < 0:
+                at(v_jobs, pos["i", c, 0] + LAG, quant, "i", c, 0, 2)
+                at(v_jobs, pos["i", c, 1] + LAG, quant, "i", c, 2, 4)
+            else:
+                at(v_jobs, pos["i", c, 1] + LAG, quant, "i", c, 0, 4)
+            done["i", c] = pos["i", c, 1] + LAG
         for c in range(NCH):
+            s0, s1 = pos["y", c, 0] + LAG, pos["y", c, 1] + LAG
+            if c == NCH - 1:
+                at(v_jobs, s0, quant, "y", c, 0, 2)
+                at(v_jobs, s0, quant, "y", c, 2, 3)
+                at(v_jobs, s1 - 1, quant, "y", c, 3, 5)
+                at(v_jobs, s1 - 1, quant, "y", c, 5, 6)
+                s1 -= 1
+            else:
+                at(v_jobs, s1, quant, "y", c, 0, 4)
+                at(v_jobs, s1, quant, "y", c, 4, 6)
+            done["y", c] = s1
             for h in range(2):
                 for r in range(RT):
-                    at(prods, pos["y", c, h] - LEAD + r, product, c, h, r)
+                    at(w_jobs, pos["y", c, h] - LEAD + r, widen, c, h, r)
+                    if c >= NA and "G" in MODE:
+                        at(g_jobs, pos["y", c, h] - LEAD + r, scale_g, c, h, r)
         t = 0
         for c in range(NCH):
-            t = qstep["i", c, 1] + 1
+            t = done["i", c] + 1
             at(pe_jobs, t, mx1, c)
             if c % 2:
                 at(s_jobs, t, empty_d, c // 2)
@@ -246,15 +305,17 @@ def tile_kktloss_pa_kernel(tc, Volt, IM, Ybr_bytes, Ybr_scale, L_limit, n_o_mu_i
         step = t + 2
         used = 0
         for c in range(NCH):
-            ready = max(step, qstep["y", c, 1] + 1)
-            at(pe_jobs, ready, mx2, c, 0)
-            at(pe_jobs, ready, mx2, c, 1)
+            ready = max(step, done["y", c] + 1)
             if c == NCH - 1:
+                ready = max(step, done["y", c] + 1)
                 for m in range(RT):
+                    at(pe_jobs, ready, mx2, c, m)
                     at(s_jobs, ready, square, c, m)
                     at(v_jobs, ready, combine, c // 2, m)
                     at(s_jobs, ready + 1, total, c // 2, m)
             else:
+                at(pe_jobs, ready, mx2, c, 0)
+                at(pe_jobs, ready, mx2, c, 1)
                 at(s_jobs, ready, square, c)
                 if c % 2 == 0:
                     at(v_jobs, ready + 1, less_limit, c // 2)
@@ -273,18 +334,20 @@ def tile_kktloss_pa_kernel(tc, Volt, IM, Ybr_bytes, Ybr_scale, L_limit, n_o_mu_i
 
         with tc.manual_schedule():
             nc.gpsimd.memset(res[:], 0.0)
-            for h in range(2):
-                nc.scalar.dma_start(out=sbc[:, h * KU:(h + 1) * KU], in_=Ybr_scale[:, h * KU:(h + 1) * KU].rearrange("o k -> (o k)").partition_broadcast(P))
+            nc.sync.dma_start(out=scol[:], in_=Ybr_scale.rearrange("o (g p t) -> p (o g) t", p=P, t=4))
             load_y(0)
             load_im(-1)
             load_im(0)
             load_y(1)
-            load_im(1)
+            if RAWB > 2:
+                load_im(1)
+            for g in range(C2):
+                spread(g)
             for s in range(-LEAD, max(n, end)):
                 if 0 <= s < n:
                     kind, c, h = seq[s]
-                    if kind == "i" and h == 0 and 0 <= c < NCH - 2:
-                        load_im(c + 2)
+                    if kind == "i" and h == 0 and 0 <= c < NCH - RAWB + 1:
+                        load_im(c + RAWB - 1)
                     if kind == "y" and h == 0 and c + 2 < NCH:
                         load_y(c + 2)
                     turn(seq[s])
@@ -292,15 +355,14 @@ def tile_kktloss_pa_kernel(tc, Volt, IM, Ybr_bytes, Ybr_scale, L_limit, n_o_mu_i
                 if 0 <= s < n:
                     empty(seq[s])
                 do(s_jobs, s)
-                do(prods, s)
-                if 0 <= s - LAG < n:
-                    quant(seq[s - LAG])
+                do(w_jobs, s)
+                do(g_jobs, s)
                 do(v_jobs, s)
                 if s == 12:
                     nc.scalar.dma_start(out=lim[:], in_=L_limit.partition_broadcast(P))
                     nc.scalar.dma_start(out=mu[:], in_=n_o_mu_i_u.rearrange("(r p) l -> p r l", p=P))
                 if s == 20:
-                    nc.gpsimd.tensor_tensor(out=lim2[:], in0=lim[:], in1=lim[:], op=ALU.mult)
+                    nc.scalar.activation(out=lim2[:], in_=lim[:], func=ACT.Square)
                 if s in (24, 30):
                     mu_total(s // 30)
 

@@ -14,361 +14,342 @@ ALU = mybir.AluOpType
 AX = mybir.AxisListType
 
 P = 128
-B, N2, NL = 256, 2048, 1536
-L2 = 2 * NL
-KP = 512
-C1, C2 = N2 // KP, L2 // KP
-ROWS = 256
-RT = 2
-NCH = L2 // ROWS
-NPAIR = NL // ROWS
-UP = 3
-KU = UP * KP
-YB = 8
-YN = 14
-TB = 5
-IB = 2
-LEAD = 3
-LAG = 2
-PER = 2
-NA = 12
-MODE = "CCG"
-GEPI = 0
-RAWB = 3
-GIB = 2
-GYB = 2
-WB = 3
-YBB = 3
+BATCH, N2, LINES = 256, 2048, 1536
+L2 = 2 * LINES
+PASS = 512
+PASSES_1, PASSES_2 = N2 // PASS, L2 // PASS
+TILES = 2
+CHUNK = TILES * P
+CHUNKS = L2 // CHUNK
+PAIRS = CHUNKS // 2
+VOLT = -1
 
-FLOPS = 2 * B * L2 * (N2 + L2)
+IM_UNIT, Y_UNIT = PASSES_1 // 2, PASSES_2 // 2
+Y_HALF = Y_UNIT * PASS
+
+Y_UNITS_EARLY = 14
+WIDEN_LEAD = 3
+QUANT_LAG = 2
+TURN_BANKS = 5
+SUM_BANKS = 8 - TURN_BANKS
+Y_CODES = 8
+FIRST_CUTS = (0, PASS, Y_HALF, L2)
+
+FLOPS = 2 * BATCH * L2 * (N2 + L2)
 
 
 def tile_kktloss_pa_kernel(tc, Volt, IM, Ybr_bytes, Ybr_scale, L_limit, n_o_mu_i_u, out):
     nc = tc.nc
     with ExitStack() as ctx:
         keep = ctx.enter_context(tc.tile_pool(name="keep", bufs=1))
-        pool = ctx.enter_context(tc.tile_pool(name="work", bufs=2))
+        work = ctx.enter_context(tc.tile_pool(name="work", bufs=2))
         psum = ctx.enter_context(tc.psum_pool(name="psum", bufs=1))
 
-        ident = keep.tile([P, P], F32, name="ident")
-        make_identity(nc, ident[:])
-        warm = keep.tile([P, 1], F32, name="warm")
-        nc.vector.memset(warm[:], 0.0)
-        warm2 = keep.tile([P, 1], F32, name="warm2")
-        nc.scalar.activation(out=warm2[:], in_=warm[:], func=ACT.Square)
+        identity = keep.tile([P, P], F32, name="identity")
+        make_identity(nc, identity[:])
 
-        scol = keep.tile([P, C2, 4], F32, name="scol")
-        sbc = keep.tile([P, L2], F32, name="sbc")
-        lim = keep.tile([P, NL], BF16, name="lim")
-        lim2 = keep.tile([P, NL], F32, name="lim2")
-        mu = keep.tile([P, RT, NL], BF16, name="mu")
-        res = keep.tile([P, P], F32, name="res")
-        sums = keep.tile([P, RT, 2 * NPAIR + 1], F32, name="sums")
-        v_codes = keep.tile([P, C1, B], U32, name="v_codes", align_bytes=64)
-        v_scales = keep.tile([P, C1, B], U8, name="v_scales", align_bytes=64)
-        d_codes = keep.tile([P, C2, B], U32, name="d_codes", align_bytes=64)
-        d_scales = keep.tile([P, C2, B], U8, name="d_scales", align_bytes=64)
+        table_in = keep.tile([P, 1], F32, name="table_in")
+        nc.vector.memset(table_in[:], 0.0)
+        table_out = keep.tile([P, 1], F32, name="table_out")
+        nc.scalar.activation(out=table_out[:], in_=table_in[:], func=ACT.Square)
 
-        volt_v = Volt.rearrange("(r p) k -> p r k", p=P)
-        im_v = IM.rearrange("(g m t) k -> g m t k", m=P, t=4)
-        y_v = Ybr_bytes.rearrange("(c r p) k -> c p r k", r=RT, p=P)
+        scale_k = keep.tile([P, PASSES_2, 4], F32, name="scale_k")
+        scale_row = keep.tile([P, L2], F32, name="scale_row")
+        limit = keep.tile([P, LINES], BF16, name="limit")
+        limit_sq = keep.tile([P, LINES], F32, name="limit_sq")
+        mu = keep.tile([P, TILES, LINES], BF16, name="mu")
+        unused = keep.tile([P, LINES], BF16, name="unused")
+        sums = keep.tile([P, TILES, 2 * PAIRS + 1], F32, name="sums")
+        totals = keep.tile([P, P], F32, name="totals")
+        totals_t = keep.tile([P, P], F32, name="totals_t")
+        volt_codes = keep.tile([P, PASSES_1, BATCH], U32, name="volt_codes", align_bytes=64)
+        volt_scales = keep.tile([P, PASSES_1, BATCH], U8, name="volt_scales", align_bytes=64)
+        d_codes = keep.tile([P, PASSES_2, BATCH], U32, name="d_codes", align_bytes=64)
+        d_scales = keep.tile([P, PASSES_2, BATCH], U8, name="d_scales", align_bytes=64)
 
-        raw, byts, wide, prod, grouped, banks, im_q, y_q = {}, {}, {}, {}, {}, {}, {}, {}
-        d_bank, d_grp, y_bank = {}, {}, {}
+        volt_rows = Volt.rearrange("(r p) k -> p r k", p=P)
+        im_rows = IM.rearrange("(g m t) k -> g m t k", m=P, t=4)
+        y_rows = Ybr_bytes.rearrange("(c r p) k -> c p r k", r=TILES, p=P)
 
-        def load_im(c):
-            raw[c] = pool.tile([P, RT, N2], BF16, name="raw", bufs=RAWB)
-            src = volt_v if c < 0 else im_v[c // 2][:, 2 * (c % 2):2 * (c % 2) + 2, :]
-            if c < 1:
-                for h in range(2):
-                    nc.sync.dma_start(out=raw[c][:, :, h * 1024:(h + 1) * 1024], in_=src[:, :, h * 1024:(h + 1) * 1024])
+        rows, y_bytes, wide, turned, grouped = {}, {}, {}, {}, {}
+        im_quant, y_quant, d_bank, d_grouped, y_bank = {}, {}, {}, {}, {}
+        sq_re, sq_im, mu_g = {}, {}, {}
+
+        def load_rows(c):
+            rows[c] = work.tile([P, TILES, N2], BF16, name="rows", bufs=3)
+            if c == VOLT:
+                src = volt_rows
             else:
-                nc.sync.dma_start(out=raw[c][:], in_=src)
-
-        def y_chunk_rows(c):
-            return c // 2 + (c % 2) * NPAIR
+                slot = TILES * (c % 2)
+                src = im_rows[c // 2][:, slot:slot + TILES, :]
+            cuts = (0, N2 // 2, N2) if c < 1 else (0, N2)
+            for a, b in zip(cuts, cuts[1:]):
+                nc.sync.dma_start(out=rows[c][:, :, a:b], in_=src[:, :, a:b])
 
         def load_y(c):
-            byts[c] = pool.tile([P, RT, L2], U8, name="ybytes", bufs=YBB)
-            cuts = (0, KU, L2) if c == 0 else (0, L2)
+            y_bytes[c] = work.tile([P, TILES, L2], U8, name="y_bytes", bufs=3)
+            src = y_rows[c // 2 + (c % 2) * PAIRS]
+            cuts = (0, Y_HALF, L2) if c == 0 else (0, L2)
             for a, b in zip(cuts, cuts[1:]):
-                nc.sync.dma_start(out=byts[c][:, :, a:b], in_=y_v[y_chunk_rows(c)][:, :, a:b])
+                nc.sync.dma_start(out=y_bytes[c][:, :, a:b], in_=src[:, :, a:b])
 
-        def spread(g):
-            bank = psum.tile([P, 4, P], F32, name="turned", bufs=TB)
+        def spread_scales(g):
+            bank = psum.tile([P, 4, P], F32, name="turned", bufs=TURN_BANKS)
             for t in range(4):
-                nc.tensor.transpose(bank[:, t, :], scol[:, g, t:t + 1].to_broadcast([P, P]), ident[:])
-            dst = sbc[:, g * KP:(g + 1) * KP].rearrange("p (n t) -> p n t", t=4)
+                nc.tensor.transpose(bank[:, t, :], scale_k[:, g, t:t + 1].to_broadcast([P, P]), identity[:])
+            dst = scale_row[:, g * PASS:(g + 1) * PASS].rearrange("p (n t) -> p n t", t=4)
             src = bank[:].rearrange("p t n -> p n t")
-            if g in (0, 2):
+            if g == 0:
                 nc.vector.tensor_copy(out=dst, in_=src)
             else:
                 nc.scalar.copy(out=dst, in_=src)
 
-        def mode(u):
-            kind, c, h = u
-            if kind == "i":
-                return "A" * 2
-            return "A" * UP if c < NA else MODE
+        def widen(c, r, a, b):
+            if r == 0 and a == 0:
+                wide[c] = work.tile([P, TILES, L2], BF16, name="wide", bufs=2)
+            nc.vector.tensor_tensor(out=wide[c][:, r, a:b], in0=y_bytes[c][:, r, a:b].bitcast(FP8), in1=scale_row[:, a:b], op=ALU.mult)
 
-        def new_wide(c, h):
-            wide[c, h] = pool.tile([P, RT, KU], BF16, name="wide", bufs=WB)
+        def unit_passes(unit):
+            kind, c, h = unit
+            n = IM_UNIT if kind == "im" else Y_UNIT
+            return range(n * h, n * h + n)
 
-        def widen(c, h, r):
-            if r == 0:
-                new_wide(c, h)
-            ks = slice(h * KU, (h + 1) * KU)
-            src = byts[c][:, r, ks].bitcast(FP8)
-            if c < NA:
-                nc.vector.tensor_tensor(out=wide[c, h][:, r, :], in0=src, in1=sbc[:, ks], op=ALU.mult)
-            else:
-                nc.scalar.copy(out=wide[c, h][:, r, :], in_=src)
-
-        def scale_g(c, h, r):
-            if r == 0:
-                prod[c, h] = pool.tile([P, RT, KP], BF16, name="prod", bufs=2)
-            j = MODE.index("G")
-            ks = slice(h * KU + j * KP, h * KU + (j + 1) * KP)
-            nc.gpsimd.tensor_tensor(out=prod[c, h][:, r, :], in0=wide[c, h][:, r, j * KP:(j + 1) * KP], in1=sbc[:, ks], op=ALU.mult)
-
-        def turn(u):
-            kind, c, h = u
-            banks[u] = []
-            for j, md in enumerate(mode(u)):
-                bank = psum.tile([P, 2, ROWS], F32, name="turned", bufs=TB)
+        def turn(unit):
+            kind, c, h = unit
+            src = rows[c] if kind == "im" else wide[c]
+            for g in unit_passes(unit):
+                bank = psum.tile([P, 2, CHUNK], F32, name="turned", bufs=TURN_BANKS)
                 for w in range(2):
-                    for r in range(RT):
-                        if kind == "i":
-                            words = raw[c][:, r, (2 * h + j) * KP:(2 * h + j + 1) * KP].bitcast(F32)
-                        elif md == "G":
-                            words = prod[c, h][:, r, :].bitcast(F32)
-                        else:
-                            words = wide[c, h][:, r, j * KP:(j + 1) * KP].bitcast(F32)
-                        nc.tensor.transpose(bank[:, w, r * P:(r + 1) * P], words[:, w::2], ident[:])
-                banks[u].append(bank)
+                    for r in range(TILES):
+                        words = src[:, r, g * PASS:(g + 1) * PASS].bitcast(F32)
+                        nc.tensor.transpose(bank[:, w, r * P:(r + 1) * P], words[:, w::2], identity[:])
+                turned[kind, c, g] = bank
 
-        def empty(u):
-            kind, c, h = u
-            n = len(banks[u])
+        def empty(unit):
+            kind, c, h = unit
             if h == 0:
-                if kind == "i":
-                    grouped[kind, c] = pool.tile([P, C1, ROWS * 4], BF16, name="grouped_i", bufs=GIB, align_bytes=64)
+                if kind == "im":
+                    grouped[kind, c] = work.tile([P, PASSES_1, CHUNK * 4], BF16, name="grouped_im", bufs=2, align_bytes=64)
                 else:
-                    grouped[kind, c] = pool.tile([P, C2, ROWS * 4], BF16, name="grouped_y", bufs=GYB, align_bytes=64)
-            for j, md in enumerate(mode(u)):
-                g = n * h + j
-                dst = grouped[kind, c][:, g, :]
-                bank = banks[u][j]
-                if md == "C":
-                    nc.vector.tensor_tensor(
-                        out=dst.rearrange("p (r w e) -> p r w e", w=2, e=2),
-                        in0=bank[:].rearrange("p w r -> p (w r)").bitcast(BF16).rearrange("p (w r e) -> p r w e", w=2, e=2),
-                        in1=scol[:, g, :].rearrange("p (w e) -> p w e", e=2).unsqueeze(1).to_broadcast([P, ROWS, 2, 2]),
-                        op=ALU.mult)
-                else:
-                    nc.scalar.copy(out=dst.bitcast(F32).rearrange("p (r w) -> p r w", w=2), in_=bank[:].rearrange("p w r -> p r w"))
+                    grouped[kind, c] = work.tile([P, PASSES_2, CHUNK * 4], BF16, name="grouped_y", bufs=2, align_bytes=64)
+            for g in unit_passes(unit):
+                dst = grouped[kind, c][:, g, :].bitcast(F32).rearrange("p (r w) -> p r w", w=2)
+                nc.scalar.copy(out=dst, in_=turned[kind, c, g][:].rearrange("p w r -> p r w"))
 
-        def quant(kind, c, a, b):
-            if kind == "i" and c < 0:
-                cq, sq = v_codes, v_scales
-            elif kind == "i":
+        def quantise(kind, c, a, b):
+            if kind == "im" and c == VOLT:
+                codes, scales = volt_codes, volt_scales
+            elif kind == "im":
                 if a == 0:
-                    im_q[c] = (pool.tile([P, C1, ROWS], U32, name="im_codes", bufs=IB, align_bytes=64),
-                               pool.tile([P, C1, ROWS], U8, name="im_scales", bufs=IB, align_bytes=64))
-                cq, sq = im_q[c]
+                    im_quant[c] = (work.tile([P, PASSES_1, CHUNK], U32, name="im_codes", bufs=2, align_bytes=64),
+                                   work.tile([P, PASSES_1, CHUNK], U8, name="im_scales", bufs=2, align_bytes=64))
+                codes, scales = im_quant[c]
             else:
                 if a == 0:
-                    y_q[c] = (pool.tile([P, C2, ROWS], U32, name="y_codes", bufs=YB, align_bytes=64),
-                              pool.tile([P, C2, ROWS], U8, name="y_scales", bufs=YB, align_bytes=64))
-                cq, sq = y_q[c]
+                    y_quant[c] = (work.tile([P, PASSES_2, CHUNK], U32, name="y_codes", bufs=Y_CODES, align_bytes=64),
+                                  work.tile([P, PASSES_2, CHUNK], U8, name="y_scales", bufs=Y_CODES, align_bytes=64))
+                codes, scales = y_quant[c]
             nc.vector.quantize_mx(
-                out=cq[:, a:b, :].rearrange("p g r -> p (g r)").bitcast(FP8X4),
-                scales=sq[:, a:b, :].rearrange("p g r -> p (g r)"),
+                out=codes[:, a:b, :].rearrange("p g r -> p (g r)").bitcast(FP8X4),
+                scales=scales[:, a:b, :].rearrange("p g r -> p (g r)"),
                 in_=grouped[kind, c][:, a:b, :].rearrange("p g k -> p (g k)"))
 
-        def mx1(c):
-            gp, odd = c // 2, c % 2
-            if odd == 0:
-                d_bank[gp] = [psum.tile([P, 4, P], F32, name="acc", bufs=8 - TB) for hb in range(2)]
-            cq, sq = im_q[c]
-            for hb in range(2):
-                bs = slice(hb * P, (hb + 1) * P)
-                for r in range(RT):
-                    rs = slice(r * P, (r + 1) * P)
-                    for g in range(C1):
+        def multiply_1(c):
+            group, first_slot = c // 2, TILES * (c % 2)
+            if first_slot == 0:
+                d_bank[group] = [psum.tile([P, 4, P], F32, name="sum", bufs=SUM_BANKS) for m in range(TILES)]
+            codes, scales = im_quant[c]
+            for m in range(TILES):
+                samples = slice(m * P, (m + 1) * P)
+                for r in range(TILES):
+                    cols = slice(r * P, (r + 1) * P)
+                    for g in range(PASSES_1):
                         nc.tensor.matmul_mx(
-                            out=d_bank[gp][hb][:, 2 * odd + r, :],
-                            lhsT=cq[:, g, rs].bitcast(FP8X4), lhsT_scale=sq[:, g, rs],
-                            rhs=v_codes[:, g, bs].bitcast(FP8X4), rhs_scale=v_scales[:, g, bs],
-                            start=(g == 0), stop=(g == C1 - 1))
+                            out=d_bank[group][m][:, first_slot + r, :],
+                            lhsT=codes[:, g, cols].bitcast(FP8X4), lhsT_scale=scales[:, g, cols],
+                            rhs=volt_codes[:, g, samples].bitcast(FP8X4), rhs_scale=volt_scales[:, g, samples],
+                            start=(g == 0), stop=(g == PASSES_1 - 1))
 
-        def empty_d(gp):
-            d_grp[gp] = pool.tile([P, B, 4], BF16, name="d_grouped", bufs=2, align_bytes=64)
-            for hb in range(2):
-                nc.scalar.copy(out=d_grp[gp][:, hb * P:(hb + 1) * P, :], in_=d_bank[gp][hb][:].rearrange("p t b -> p b t"))
+        def empty_d(group):
+            d_grouped[group] = work.tile([P, BATCH, 4], BF16, name="d_grouped", bufs=2, align_bytes=64)
+            for m in range(TILES):
+                nc.scalar.copy(out=d_grouped[group][:, m * P:(m + 1) * P, :], in_=d_bank[group][m][:].rearrange("p t b -> p b t"))
 
-        def quant_d(gp):
-            nc.vector.quantize_mx(out=d_codes[:, gp, :].bitcast(FP8X4), scales=d_scales[:, gp, :], in_=d_grp[gp][:].rearrange("p b t -> p (b t)"))
+        def quantise_d(group):
+            nc.vector.quantize_mx(out=d_codes[:, group, :].bitcast(FP8X4), scales=d_scales[:, group, :],
+                                  in_=d_grouped[group][:].rearrange("p b t -> p (b t)"))
 
-        def mx2(c, m, ga=0, gb=C2):
-            if m == 0 and ga == 0:
-                y_bank[c] = psum.tile([P, RT, ROWS], F32, name="acc", bufs=8 - TB)
-            cq, sq = y_q[c]
-            ms = slice(m * P, (m + 1) * P)
-            for g in range(ga, gb):
+        def multiply_2(c, m, a, b):
+            last = c == CHUNKS - 1
+            if last and a == 0:
+                y_bank[c, m] = psum.tile([P, CHUNK], F32, name="sum", bufs=SUM_BANKS)
+            elif not last and m == 0:
+                y_bank[c] = psum.tile([P, TILES, CHUNK], F32, name="sum", bufs=SUM_BANKS)
+            codes, scales = y_quant[c]
+            samples = slice(m * P, (m + 1) * P)
+            for g in range(a, b):
                 nc.tensor.matmul_mx(
-                    out=y_bank[c][:, m, :],
-                    lhsT=d_codes[:, g, ms].bitcast(FP8X4), lhsT_scale=d_scales[:, g, ms],
-                    rhs=cq[:, g, :].bitcast(FP8X4), rhs_scale=sq[:, g, :],
-                    start=(g == 0), stop=(g == C2 - 1))
+                    out=y_bank[c, m][:] if last else y_bank[c][:, m, :],
+                    lhsT=d_codes[:, g, samples].bitcast(FP8X4), lhsT_scale=d_scales[:, g, samples],
+                    rhs=codes[:, g, :].bitcast(FP8X4), rhs_scale=scales[:, g, :],
+                    start=(g == 0), stop=(g == PASSES_2 - 1))
 
-        sq_t, u_t = {}, {}
+        def load_limits():
+            nc.scalar.dma_start(out=limit[:], in_=L_limit.partition_broadcast(P))
+            nc.scalar.dma_start(out=mu[:], in_=n_o_mu_i_u.rearrange("(r p) l -> p r l", p=P))
 
-        def square(c, m=None):
-            if m is None or m == 0:
-                sq_t[c] = pool.tile([P, RT, ROWS], F32, name="sq_im" if c % 2 else "sq_re", bufs=2)
-            sl = slice(None) if m is None else slice(m, m + 1)
-            nc.scalar.activation(out=sq_t[c][:, sl, :], in_=y_bank[c][:, sl, :], func=ACT.Square)
+        def square_limit():
+            nc.scalar.activation(out=limit_sq[:], in_=limit[:], func=ACT.Square)
 
-        def two_input(i):
-            return nc.gpsimd if i < GEPI else nc.vector
+        def square_re(i):
+            sq_re[i] = work.tile([P, TILES, CHUNK], F32, name="sq_re", bufs=2)
+            nc.scalar.activation(out=sq_re[i][:], in_=y_bank[2 * i][:], func=ACT.Square)
 
-        def less_limit(i):
-            ls = slice(i * ROWS, (i + 1) * ROWS)
-            two_input(i).tensor_tensor(out=sq_t[2 * i][:], in0=sq_t[2 * i][:], in1=lim2[:, ls].unsqueeze(1).to_broadcast([P, RT, ROWS]), op=ALU.subtract)
+        def subtract_limit(i):
+            lines = limit_sq[:, i * CHUNK:(i + 1) * CHUNK].unsqueeze(1).to_broadcast([P, TILES, CHUNK])
+            nc.vector.tensor_tensor(out=sq_re[i][:], in0=sq_re[i][:], in1=lines, op=ALU.subtract)
 
-        def combine(i, m=None):
-            ls = slice(i * ROWS, (i + 1) * ROWS)
-            if m is None or m == 0:
-                u_t[i] = pool.tile([P, RT, ROWS], F32, name="u_t", bufs=2)
-            sl = slice(None) if m is None else slice(m, m + 1)
-            two_input(i).tensor_tensor(out=sq_t[2 * i][:, sl, :], in0=sq_t[2 * i][:, sl, :], in1=sq_t[2 * i + 1][:, sl, :], op=ALU.add)
-            two_input(i).tensor_tensor(out=u_t[i][:, sl, :], in0=sq_t[2 * i][:, sl, :], in1=mu[:, sl, ls], op=ALU.mult)
-
-        def total(i, m):
-            nc.scalar.activation(out=sq_t[2 * i][:, m, :], in_=sq_t[2 * i][:, m, :], func=ACT.Relu, accum_out=sums[:, m, 2 * i:2 * i + 1])
-            nc.scalar.activation(out=u_t[i][:, m, :], in_=u_t[i][:, m, :], func=ACT.Abs, accum_out=sums[:, m, 2 * i + 1:2 * i + 2])
-
-        def mu_total(m):
-            nc.scalar.activation(out=lim[:], in_=mu[:, m, :], func=ACT.Relu, scale=-1.0, accum_out=sums[:, m, 2 * NPAIR:2 * NPAIR + 1])
-
-        im_u = [("i", c, h) for c in range(NCH) for h in range(2)]
-        y_u = [("y", c, h) for c in range(NCH) for h in range(2)]
-        seq = [("i", -1, 0), ("i", -1, 1)]
-        ny = 0
-        for k, u in enumerate(im_u):
-            seq.append(u)
-            if (k + 1) * YN // 24 > ny:
-                seq.append(y_u[ny])
-                ny += 1
-        seq += y_u[ny:]
-        n = len(seq)
-        pos = {u: s for s, u in enumerate(seq)}
-
-        pe_jobs, s_jobs, v_jobs, g_jobs, w_jobs = {}, {}, {}, {}, {}
-
-        def at(table, step, fn, *args):
-            table.setdefault(step, []).append((fn, args))
-
-        done = {}
-        for c in range(-1, NCH):
-            if c < 0:
-                at(v_jobs, pos["i", c, 0] + LAG, quant, "i", c, 0, 2)
-                at(v_jobs, pos["i", c, 1] + LAG, quant, "i", c, 2, 4)
+        def square_im(i):
+            sq_im[i] = work.tile([P, TILES, CHUNK], F32, name="sq_im", bufs=2)
+            if i < PAIRS - 1:
+                nc.scalar.activation(out=sq_im[i][:], in_=y_bank[2 * i + 1][:], func=ACT.Square)
             else:
-                at(v_jobs, pos["i", c, 1] + LAG, quant, "i", c, 0, 4)
-            done["i", c] = pos["i", c, 1] + LAG
-        for c in range(NCH):
-            s0, s1 = pos["y", c, 0] + LAG, pos["y", c, 1] + LAG
-            if c == NCH - 1:
-                at(v_jobs, s0, quant, "y", c, 0, 2)
-                at(v_jobs, s0, quant, "y", c, 2, 3)
-                at(v_jobs, s1 - 1, quant, "y", c, 3, 5)
-                at(v_jobs, s1 - 1, quant, "y", c, 5, 6)
-                s1 -= 1
-            else:
-                at(v_jobs, s1, quant, "y", c, 0, 4)
-                at(v_jobs, s1, quant, "y", c, 4, 6)
-            done["y", c] = s1
-            for h in range(2):
-                for r in range(RT):
-                    at(w_jobs, pos["y", c, h] - LEAD + r, widen, c, h, r)
-                    if c >= NA and "G" in MODE:
-                        at(g_jobs, pos["y", c, h] - LEAD + r, scale_g, c, h, r)
-        t = 0
-        for c in range(NCH):
-            t = done["i", c] + 1
-            at(pe_jobs, t, mx1, c)
-            if c % 2:
-                at(s_jobs, t, empty_d, c // 2)
-                at(v_jobs, t + 1, quant_d, c // 2)
-        step = t + 2
-        used = 0
-        for c in range(NCH):
-            ready = max(step, done["y", c] + 1)
-            if c == NCH - 1:
-                ready = max(step, done["y", c] + 1)
-                for m in range(RT):
-                    at(pe_jobs, ready, mx2, c, m)
-                    at(s_jobs, ready, square, c, m)
-                    at(v_jobs, ready, combine, c // 2, m)
-                    at(s_jobs, ready + 1, total, c // 2, m)
-            else:
-                at(pe_jobs, ready, mx2, c, 0)
-                at(pe_jobs, ready, mx2, c, 1)
-                at(s_jobs, ready, square, c)
-                if c % 2 == 0:
-                    at(v_jobs, ready + 1, less_limit, c // 2)
-                else:
-                    at(v_jobs, ready + 1, combine, c // 2)
-                    at(s_jobs, ready + 2, total, c // 2, 0)
-                    at(s_jobs, ready + 2, total, c // 2, 1)
-            used = used + 1 if ready == step else 1
-            step = ready + (used == PER)
-            used = 0 if used == PER else used
-        end = max(max(pe_jobs), max(s_jobs), max(v_jobs)) + 1
+                for m in range(TILES):
+                    nc.scalar.activation(out=sq_im[i][:, m, :], in_=y_bank[2 * i + 1, m][:], func=ACT.Square)
 
-        def do(table, s):
-            for fn, args in table.get(s, []):
+        def combine(i, ms):
+            if i not in mu_g:
+                mu_g[i] = work.tile([P, TILES, CHUNK], F32, name="mu_g", bufs=2)
+            nc.vector.tensor_tensor(out=sq_re[i][:, ms, :], in0=sq_re[i][:, ms, :], in1=sq_im[i][:, ms, :], op=ALU.add)
+            nc.vector.tensor_tensor(out=mu_g[i][:, ms, :], in0=sq_re[i][:, ms, :], in1=mu[:, ms, i * CHUNK:(i + 1) * CHUNK], op=ALU.mult)
+
+        def add_up(i):
+            for m in range(TILES):
+                for j, (t, func) in enumerate(((sq_re[i], ACT.Relu), (mu_g[i], ACT.Abs))):
+                    nc.scalar.activation(out=t[:, m, :], in_=t[:, m, :], func=func, accum_out=sums[:, m, 2 * i + j:2 * i + j + 1])
+
+        def add_up_mu(m):
+            nc.scalar.activation(out=unused[:], in_=mu[:, m, :], func=ACT.Relu, scale=-1.0, accum_out=sums[:, m, 2 * PAIRS:2 * PAIRS + 1])
+
+        y_units = [("y", c, h) for c in range(CHUNKS) for h in range(2)]
+        order = [("im", VOLT, 0), ("im", VOLT, 1)]
+        taken = 0
+        for k in range(2 * CHUNKS):
+            order.append(("im", k // 2, k % 2))
+            if (k + 1) * Y_UNITS_EARLY // (2 * CHUNKS) > taken:
+                order.append(y_units[taken])
+                taken += 1
+        order += y_units[taken:]
+        step_of = {unit: s for s, unit in enumerate(order)}
+
+        tensor_jobs, scalar_jobs, vector_jobs = {}, {}, {}
+
+        def at(jobs, step, fn, *args):
+            jobs.setdefault(step, []).append((fn, args))
+
+        def do(jobs, step):
+            for fn, args in jobs.get(step, []):
                 fn(*args)
 
-        with tc.manual_schedule():
-            nc.gpsimd.memset(res[:], 0.0)
-            nc.sync.dma_start(out=scol[:], in_=Ybr_scale.rearrange("o (g p t) -> p (o g) t", p=P, t=4))
-            load_y(0)
-            load_im(-1)
-            load_im(0)
-            load_y(1)
-            if RAWB > 2:
-                load_im(1)
-            for g in range(C2):
-                spread(g)
-            for s in range(-LEAD, max(n, end)):
-                if 0 <= s < n:
-                    kind, c, h = seq[s]
-                    if kind == "i" and h == 0 and 0 <= c < NCH - RAWB + 1:
-                        load_im(c + RAWB - 1)
-                    if kind == "y" and h == 0 and c + 2 < NCH:
-                        load_y(c + 2)
-                    turn(seq[s])
-                do(pe_jobs, s)
-                if 0 <= s < n:
-                    empty(seq[s])
-                do(s_jobs, s)
-                do(w_jobs, s)
-                do(g_jobs, s)
-                do(v_jobs, s)
-                if s == 12:
-                    nc.scalar.dma_start(out=lim[:], in_=L_limit.partition_broadcast(P))
-                    nc.scalar.dma_start(out=mu[:], in_=n_o_mu_i_u.rearrange("(r p) l -> p r l", p=P))
-                if s == 20:
-                    nc.scalar.activation(out=lim2[:], in_=lim[:], func=ACT.Square)
-                if s in (24, 30):
-                    mu_total(s // 30)
+        for a, b in zip(FIRST_CUTS, FIRST_CUTS[1:]):
+            for r in range(TILES):
+                at(vector_jobs, -WIDEN_LEAD if b <= Y_HALF else 1 + r - WIDEN_LEAD, widen, 0, r, a, b)
+        for c in range(1, CHUNKS - 1):
+            for r in range(TILES):
+                at(vector_jobs, step_of["y", c, 0] - WIDEN_LEAD + 2 * r, widen, c, r, 0, L2)
+        for h in range(2):
+            for r in range(TILES):
+                c = CHUNKS - 1
+                at(vector_jobs, step_of["y", c, h] - WIDEN_LEAD + r, widen, c, r, h * Y_HALF, (h + 1) * Y_HALF)
 
-            nc.vector.tensor_reduce(out=res[:, 0:RT], in_=sums[:], axis=AX.X, op=ALU.add)
-            fin = psum.tile([P, P], F32, name="acc", bufs=8 - TB)
-            nc.tensor.transpose(fin[:], res[:], ident[:])
-            fin_sb = keep.tile([P, P], F32, name="fin_sb")
-            nc.vector.tensor_copy(out=fin_sb[:], in_=fin[:])
-            nc.sync.dma_start(out=out.rearrange("(m p) -> m p", p=P), in_=fin_sb[0:RT, :])
+        quantised = {}
+        for c in range(VOLT, CHUNKS):
+            done = step_of["im", c, 1] + QUANT_LAG
+            if c == VOLT:
+                at(vector_jobs, done - 1, quantise, "im", c, 0, IM_UNIT)
+                at(vector_jobs, done, quantise, "im", c, IM_UNIT, PASSES_1)
+            else:
+                at(vector_jobs, done, quantise, "im", c, 0, PASSES_1)
+            quantised["im", c] = done
+        for c in range(CHUNKS - 1):
+            done = step_of["y", c, 1] + QUANT_LAG
+            at(vector_jobs, done, quantise, "y", c, 0, 4)
+            at(vector_jobs, done, quantise, "y", c, 4, PASSES_2)
+            quantised["y", c] = done
+        c = CHUNKS - 1
+        done = step_of["y", c, 1] + 1
+        for h in range(2):
+            at(vector_jobs, done, quantise, "y", c, 3 * h, 3 * h + 2)
+            at(vector_jobs, done, quantise, "y", c, 3 * h + 2, 3 * h + 3)
+        quantised["y", c] = done
+
+        for c in range(CHUNKS):
+            step = quantised["im", c] + 1
+            at(tensor_jobs, step, multiply_1, c)
+            if c % 2:
+                at(scalar_jobs, step, empty_d, c // 2)
+                at(vector_jobs, step + (2 if c < CHUNKS - 1 else 1), quantise_d, c // 2)
+
+        step, in_step = step + 2, 0
+        for c in range(CHUNKS):
+            ready = max(step, quantised["y", c] + 1)
+            if c < CHUNKS - 1:
+                for m in range(TILES):
+                    at(tensor_jobs, ready, multiply_2, c, m, 0, PASSES_2)
+            else:
+                for a, b in ((0, PASSES_2 - 1), (PASSES_2 - 1, PASSES_2)):
+                    for m in range(TILES):
+                        at(tensor_jobs, ready, multiply_2, c, m, a, b)
+            if c % 2 == 0:
+                at(scalar_jobs, ready, square_re, c // 2)
+                at(vector_jobs, ready + 1, subtract_limit, c // 2)
+            elif c < CHUNKS - 1:
+                at(scalar_jobs, ready, square_im, c // 2)
+                at(vector_jobs, ready + 1, combine, c // 2, slice(0, TILES))
+                at(scalar_jobs, ready + 2, add_up, c // 2)
+            else:
+                at(scalar_jobs, ready, square_im, c // 2)
+                for m in range(TILES):
+                    at(vector_jobs, ready, combine, c // 2, slice(m, m + 1))
+                at(scalar_jobs, ready + 1, add_up, c // 2)
+            in_step = in_step + 1 if ready == step else 1
+            step = ready + in_step // 2
+            in_step = in_step % 2
+        steps = ready + 2
+
+        at(scalar_jobs, 12, load_limits)
+        at(scalar_jobs, 20, square_limit)
+        for m in range(TILES):
+            at(scalar_jobs, 24 + 6 * m, add_up_mu, m)
+
+        with tc.manual_schedule():
+            nc.gpsimd.memset(totals[:], 0.0)
+            nc.sync.dma_start(out=scale_k[:], in_=Ybr_scale.rearrange("o (g p t) -> p (o g) t", p=P, t=4))
+            load_y(0)
+            load_rows(VOLT)
+            load_rows(0)
+            load_y(1)
+            load_rows(1)
+            for g in range(PASSES_2):
+                spread_scales(g)
+            for step in range(-WIDEN_LEAD, steps):
+                unit = order[step] if 0 <= step < len(order) else None
+                if unit:
+                    kind, c, h = unit
+                    if h == 0 and 0 <= c < CHUNKS - 2:
+                        if kind == "im":
+                            load_rows(c + 2)
+                        else:
+                            load_y(c + 2)
+                    turn(unit)
+                do(tensor_jobs, step)
+                if unit:
+                    empty(unit)
+                do(scalar_jobs, step)
+                do(vector_jobs, step)
+
+            nc.vector.tensor_reduce(out=totals[:, 0:TILES], in_=sums[:], axis=AX.X, op=ALU.add)
+            bank = psum.tile([P, P], F32, name="sum", bufs=SUM_BANKS)
+            nc.tensor.transpose(bank[:], totals[:], identity[:])
+            nc.vector.tensor_copy(out=totals_t[:], in_=bank[:])
+            nc.sync.dma_start(out=out.rearrange("(m p) -> m p", p=P), in_=totals_t[0:TILES, :])

@@ -29,7 +29,11 @@ Y_HALF = Y_UNIT * PASS
 
 Y_UNITS_EARLY = 14
 WIDEN_LEAD = 3
+TILE_LAG = 2
+CAST_LEAD = 2
 QUANT_LAG = 2
+D_LAG = 2
+SCALAR_CHUNKS = (6, 8, 9)
 TURN_BANKS = 5
 SUM_BANKS = 8 - TURN_BANKS
 Y_CODES = 8
@@ -109,6 +113,18 @@ def tile_kktloss_pa_kernel(tc, Volt, IM, Ybr_bytes, Ybr_scale, L_limit, n_o_mu_i
                 wide[c] = work.tile([P, TILES, L2], BF16, name="wide", bufs=2)
             nc.vector.tensor_tensor(out=wide[c][:, r, a:b], in0=y_bytes[c][:, r, a:b].bitcast(FP8), in1=scale_row[:, a:b], op=ALU.mult)
 
+        def vector_cols(c):
+            return L2 - PASS if c in SCALAR_CHUNKS else L2
+
+        def cast_last_pass(c):
+            for r in range(TILES):
+                nc.scalar.copy(out=wide[c][:, r, L2 - PASS:L2], in_=y_bytes[c][:, r, L2 - PASS:L2].bitcast(FP8))
+
+        def scale_and_empty(bank, g, dst):
+            for t in range(4):
+                pairs = bank[:, t // 2, :].bitcast(BF16).rearrange("p (r e) -> p r e", e=2)
+                nc.scalar.activation(out=dst.rearrange("p (r t) -> p r t", t=4)[:, :, t], in_=pairs[:, :, t % 2], func=ACT.Copy, scale=scale_k[:, g, t:t + 1])
+
         def unit_passes(unit):
             kind, c, h = unit
             n = IM_UNIT if kind == "im" else Y_UNIT
@@ -133,8 +149,11 @@ def tile_kktloss_pa_kernel(tc, Volt, IM, Ybr_bytes, Ybr_scale, L_limit, n_o_mu_i
                 else:
                     grouped[kind, c] = work.tile([P, PASSES_2, CHUNK * 4], BF16, name="grouped_y", bufs=2, align_bytes=64)
             for g in unit_passes(unit):
-                dst = grouped[kind, c][:, g, :].bitcast(F32).rearrange("p (r w) -> p r w", w=2)
-                nc.scalar.copy(out=dst, in_=turned[kind, c, g][:].rearrange("p w r -> p r w"))
+                dst = grouped[kind, c][:, g, :]
+                if kind == "y" and g * PASS >= vector_cols(c):
+                    scale_and_empty(turned[kind, c, g], g, dst)
+                else:
+                    nc.scalar.copy(out=dst.bitcast(F32).rearrange("p (r w) -> p r w", w=2), in_=turned[kind, c, g][:].rearrange("p w r -> p r w"))
 
         def quantise(kind, c, a, b):
             if kind == "im" and c == VOLT:
@@ -256,7 +275,7 @@ def tile_kktloss_pa_kernel(tc, Volt, IM, Ybr_bytes, Ybr_scale, L_limit, n_o_mu_i
                 at(vector_jobs, -WIDEN_LEAD if b <= Y_HALF else 1 + r - WIDEN_LEAD, widen, 0, r, a, b)
         for c in range(1, CHUNKS - 1):
             for r in range(TILES):
-                at(vector_jobs, step_of["y", c, 0] - WIDEN_LEAD + 2 * r, widen, c, r, 0, L2)
+                at(vector_jobs, step_of["y", c, 0] - WIDEN_LEAD + TILE_LAG * r, widen, c, r, 0, vector_cols(c))
         for h in range(2):
             for r in range(TILES):
                 c = CHUNKS - 1
@@ -288,7 +307,7 @@ def tile_kktloss_pa_kernel(tc, Volt, IM, Ybr_bytes, Ybr_scale, L_limit, n_o_mu_i
             at(tensor_jobs, step, multiply_1, c)
             if c % 2:
                 at(scalar_jobs, step, empty_d, c // 2)
-                at(vector_jobs, step + (2 if c < CHUNKS - 1 else 1), quantise_d, c // 2)
+                at(vector_jobs, step + (D_LAG if c < CHUNKS - 1 else 1), quantise_d, c // 2)
 
         step, in_step = step + 2, 0
         for c in range(CHUNKS):
@@ -317,6 +336,8 @@ def tile_kktloss_pa_kernel(tc, Volt, IM, Ybr_bytes, Ybr_scale, L_limit, n_o_mu_i
             in_step = in_step % 2
         steps = ready + 2
 
+        for c in SCALAR_CHUNKS:
+            at(scalar_jobs, step_of["y", c, 1] - CAST_LEAD, cast_last_pass, c)
         at(scalar_jobs, 12, load_limits)
         at(scalar_jobs, 20, square_limit)
         for m in range(TILES):

from contextlib import ExitStack

import concourse.mybir as mybir
from concourse.masks import make_identity

F32 = mybir.dt.float32
BF16 = mybir.dt.bfloat16
U32 = mybir.dt.uint32
U8 = mybir.dt.uint8
FP8 = mybir.dt.float8_e4m3fn
FP8X4 = mybir.dt.float8_e4m3fn_x4
ACT = mybir.ActivationFunctionType
ALU = mybir.AluOpType
AX = mybir.AxisListType

P = 128
BATCH, N2, LINES = 256, 2048, 1536
L2 = 2 * LINES
PASS = 512
PASSES_1, PASSES_2 = N2 // PASS, L2 // PASS
TILES = 2
CHUNK = TILES * P
CHUNKS = L2 // CHUNK
PAIRS = CHUNKS // 2
VOLT = -1

IM_UNIT, Y_UNIT = PASSES_1 // 2, PASSES_2 // 2
Y_HALF = Y_UNIT * PASS

Y_UNITS_EARLY = 14
WIDEN_LEAD = 3
TILE_LAG = 2
CAST_LEAD = 2
QUANT_LAG = 2
D_LAG = 2
SCALAR_CHUNKS = (6, 8, 9)
TURN_BANKS = 5
SUM_BANKS = 8 - TURN_BANKS
Y_CODES = 8
FIRST_CUTS = (0, PASS, Y_HALF, L2)

FLOPS = 2 * BATCH * L2 * (N2 + L2)


def tile_kktloss_pa_kernel(tc, Volt, IM, Ybr_bytes, Ybr_scale, L_limit, n_o_mu_i_u, out):
    nc = tc.nc
    with ExitStack() as ctx:
        keep = ctx.enter_context(tc.tile_pool(name="keep", bufs=1))
        work = ctx.enter_context(tc.tile_pool(name="work", bufs=2))
        psum = ctx.enter_context(tc.psum_pool(name="psum", bufs=1))

        identity = keep.tile([P, P], F32, name="identity")
        make_identity(nc, identity[:])

        table_in = keep.tile([P, 1], F32, name="table_in")
        nc.vector.memset(table_in[:], 0.0)
        table_out = keep.tile([P, 1], F32, name="table_out")
        nc.scalar.activation(out=table_out[:], in_=table_in[:], func=ACT.Square)

        scale_k = keep.tile([P, PASSES_2, 4], F32, name="scale_k")
        scale_row = keep.tile([P, L2], F32, name="scale_row")
        limit = keep.tile([P, LINES], BF16, name="limit")
        limit_sq = keep.tile([P, LINES], F32, name="limit_sq")
        mu = keep.tile([P, TILES, LINES], BF16, name="mu")
        unused = keep.tile([P, LINES], BF16, name="unused")
        sums = keep.tile([P, TILES, 2 * PAIRS + 1], F32, name="sums")
        totals = keep.tile([P, P], F32, name="totals")
        totals_t = keep.tile([P, P], F32, name="totals_t")
        volt_codes = keep.tile([P, PASSES_1, BATCH], U32, name="volt_codes", align_bytes=64)
        volt_scales = keep.tile([P, PASSES_1, BATCH], U8, name="volt_scales", align_bytes=64)
        d_codes = keep.tile([P, PASSES_2, BATCH], U32, name="d_codes", align_bytes=64)
        d_scales = keep.tile([P, PASSES_2, BATCH], U8, name="d_scales", align_bytes=64)

        volt_rows = Volt.rearrange("(r p) k -> p r k", p=P)
        im_rows = IM.rearrange("(g m t) k -> g m t k", m=P, t=4)
        y_rows = Ybr_bytes.rearrange("(c r p) k -> c p r k", r=TILES, p=P)

        rows, y_bytes, wide, turned, grouped = {}, {}, {}, {}, {}
        im_quant, y_quant, d_bank, d_grouped, y_bank = {}, {}, {}, {}, {}
        sq_re, sq_im, mu_g = {}, {}, {}

        def load_rows(c):
            rows[c] = work.tile([P, TILES, N2], BF16, name="rows", bufs=3)
            if c == VOLT:
                src = volt_rows
            else:
                slot = TILES * (c % 2)
                src = im_rows[c // 2][:, slot:slot + TILES, :]
            cuts = (0, N2 // 2, N2) if c < 1 else (0, N2)
            for a, b in zip(cuts, cuts[1:]):
                nc.sync.dma_start(out=rows[c][:, :, a:b], in_=src[:, :, a:b])

        def load_y(c):
            y_bytes[c] = work.tile([P, TILES, L2], U8, name="y_bytes", bufs=3)
            src = y_rows[c // 2 + (c % 2) * PAIRS]
            cuts = (0, Y_HALF, L2) if c == 0 else (0, L2)
            for a, b in zip(cuts, cuts[1:]):
                nc.sync.dma_start(out=y_bytes[c][:, :, a:b], in_=src[:, :, a:b])

        def spread_scales(g):
            bank = psum.tile([P, 4, P], F32, name="turned", bufs=TURN_BANKS)
            for t in range(4):
                nc.tensor.transpose(bank[:, t, :], scale_k[:, g, t:t + 1].to_broadcast([P, P]), identity[:])
            dst = scale_row[:, g * PASS:(g + 1) * PASS].rearrange("p (n t) -> p n t", t=4)
            src = bank[:].rearrange("p t n -> p n t")
            if g == 0:
                nc.vector.tensor_copy(out=dst, in_=src)
            else:
                nc.scalar.copy(out=dst, in_=src)

        def widen(c, r, a, b):
            if r == 0 and a == 0:
                wide[c] = work.tile([P, TILES, L2], BF16, name="wide", bufs=2)
            nc.vector.tensor_tensor(out=wide[c][:, r, a:b], in0=y_bytes[c][:, r, a:b].bitcast(FP8), in1=scale_row[:, a:b], op=ALU.mult)

        def vector_cols(c):
            return L2 - PASS if c in SCALAR_CHUNKS else L2

        def cast_last_pass(c):
            for r in range(TILES):
                nc.scalar.copy(out=wide[c][:, r, L2 - PASS:L2], in_=y_bytes[c][:, r, L2 - PASS:L2].bitcast(FP8))

        def scale_and_empty(bank, g, dst):
            for t in range(4):
                pairs = bank[:, t // 2, :].bitcast(BF16).rearrange("p (r e) -> p r e", e=2)
                nc.scalar.activation(out=dst.rearrange("p (r t) -> p r t", t=4)[:, :, t], in_=pairs[:, :, t % 2], func=ACT.Copy, scale=scale_k[:, g, t:t + 1])

        def unit_passes(unit):
            kind, c, h = unit
            n = IM_UNIT if kind == "im" else Y_UNIT
            return range(n * h, n * h + n)

        def turn(unit):
            kind, c, h = unit
            src = rows[c] if kind == "im" else wide[c]
            for g in unit_passes(unit):
                bank = psum.tile([P, 2, CHUNK], F32, name="turned", bufs=TURN_BANKS)
                for w in range(2):
                    for r in range(TILES):
                        words = src[:, r, g * PASS:(g + 1) * PASS].bitcast(F32)
                        nc.tensor.transpose(bank[:, w, r * P:(r + 1) * P], words[:, w::2], identity[:])
                turned[kind, c, g] = bank

        def empty(unit):
            kind, c, h = unit
            if h == 0:
                if kind == "im":
                    grouped[kind, c] = work.tile([P, PASSES_1, CHUNK * 4], BF16, name="grouped_im", bufs=2, align_bytes=64)
                else:
                    grouped[kind, c] = work.tile([P, PASSES_2, CHUNK * 4], BF16, name="grouped_y", bufs=2, align_bytes=64)
            for g in unit_passes(unit):
                dst = grouped[kind, c][:, g, :]
                if kind == "y" and g * PASS >= vector_cols(c):
                    scale_and_empty(turned[kind, c, g], g, dst)
                else:
                    nc.scalar.copy(out=dst.bitcast(F32).rearrange("p (r w) -> p r w", w=2), in_=turned[kind, c, g][:].rearrange("p w r -> p r w"))

        def quantise(kind, c, a, b):
            if kind == "im" and c == VOLT:
                codes, scales = volt_codes, volt_scales
            elif kind == "im":
                if a == 0:
                    im_quant[c] = (work.tile([P, PASSES_1, CHUNK], U32, name="im_codes", bufs=2, align_bytes=64),
                                   work.tile([P, PASSES_1, CHUNK], U8, name="im_scales", bufs=2, align_bytes=64))
                codes, scales = im_quant[c]
            else:
                if a == 0:
                    y_quant[c] = (work.tile([P, PASSES_2, CHUNK], U32, name="y_codes", bufs=Y_CODES, align_bytes=64),
                                  work.tile([P, PASSES_2, CHUNK], U8, name="y_scales", bufs=Y_CODES, align_bytes=64))
                codes, scales = y_quant[c]
            nc.vector.quantize_mx(
                out=codes[:, a:b, :].rearrange("p g r -> p (g r)").bitcast(FP8X4),
                scales=scales[:, a:b, :].rearrange("p g r -> p (g r)"),
                in_=grouped[kind, c][:, a:b, :].rearrange("p g k -> p (g k)"))

        def multiply_1(c):
            group, first_slot = c // 2, TILES * (c % 2)
            if first_slot == 0:
                d_bank[group] = [psum.tile([P, 4, P], F32, name="sum", bufs=SUM_BANKS) for m in range(TILES)]
            codes, scales = im_quant[c]
            for m in range(TILES):
                samples = slice(m * P, (m + 1) * P)
                for r in range(TILES):
                    cols = slice(r * P, (r + 1) * P)
                    for g in range(PASSES_1):
                        nc.tensor.matmul_mx(
                            out=d_bank[group][m][:, first_slot + r, :],
                            lhsT=codes[:, g, cols].bitcast(FP8X4), lhsT_scale=scales[:, g, cols],
                            rhs=volt_codes[:, g, samples].bitcast(FP8X4), rhs_scale=volt_scales[:, g, samples],
                            start=(g == 0), stop=(g == PASSES_1 - 1))

        def empty_d(group):
            d_grouped[group] = work.tile([P, BATCH, 4], BF16, name="d_grouped", bufs=2, align_bytes=64)
            for m in range(TILES):
                nc.scalar.copy(out=d_grouped[group][:, m * P:(m + 1) * P, :], in_=d_bank[group][m][:].rearrange("p t b -> p b t"))

        def quantise_d(group):
            nc.vector.quantize_mx(out=d_codes[:, group, :].bitcast(FP8X4), scales=d_scales[:, group, :],
                                  in_=d_grouped[group][:].rearrange("p b t -> p (b t)"))

        def multiply_2(c, m, a, b):
            last = c == CHUNKS - 1
            if last and a == 0:
                y_bank[c, m] = psum.tile([P, CHUNK], F32, name="sum", bufs=SUM_BANKS)
            elif not last and m == 0:
                y_bank[c] = psum.tile([P, TILES, CHUNK], F32, name="sum", bufs=SUM_BANKS)
            codes, scales = y_quant[c]
            samples = slice(m * P, (m + 1) * P)
            for g in range(a, b):
                nc.tensor.matmul_mx(
                    out=y_bank[c, m][:] if last else y_bank[c][:, m, :],
                    lhsT=d_codes[:, g, samples].bitcast(FP8X4), lhsT_scale=d_scales[:, g, samples],
                    rhs=codes[:, g, :].bitcast(FP8X4), rhs_scale=scales[:, g, :],
                    start=(g == 0), stop=(g == PASSES_2 - 1))

        def load_limits():
            nc.scalar.dma_start(out=limit[:], in_=L_limit.partition_broadcast(P))
            nc.scalar.dma_start(out=mu[:], in_=n_o_mu_i_u.rearrange("(r p) l -> p r l", p=P))

        def square_limit():
            nc.scalar.activation(out=limit_sq[:], in_=limit[:], func=ACT.Square)

        def square_re(i):
            sq_re[i] = work.tile([P, TILES, CHUNK], F32, name="sq_re", bufs=2)
            nc.scalar.activation(out=sq_re[i][:], in_=y_bank[2 * i][:], func=ACT.Square)

        def subtract_limit(i):
            lines = limit_sq[:, i * CHUNK:(i + 1) * CHUNK].unsqueeze(1).to_broadcast([P, TILES, CHUNK])
            nc.vector.tensor_tensor(out=sq_re[i][:], in0=sq_re[i][:], in1=lines, op=ALU.subtract)

        def square_im(i):
            sq_im[i] = work.tile([P, TILES, CHUNK], F32, name="sq_im", bufs=2)
            if i < PAIRS - 1:
                nc.scalar.activation(out=sq_im[i][:], in_=y_bank[2 * i + 1][:], func=ACT.Square)
            else:
                for m in range(TILES):
                    nc.scalar.activation(out=sq_im[i][:, m, :], in_=y_bank[2 * i + 1, m][:], func=ACT.Square)

        def combine(i, ms):
            if i not in mu_g:
                mu_g[i] = work.tile([P, TILES, CHUNK], F32, name="mu_g", bufs=2)
            nc.vector.tensor_tensor(out=sq_re[i][:, ms, :], in0=sq_re[i][:, ms, :], in1=sq_im[i][:, ms, :], op=ALU.add)
            nc.vector.tensor_tensor(out=mu_g[i][:, ms, :], in0=sq_re[i][:, ms, :], in1=mu[:, ms, i * CHUNK:(i + 1) * CHUNK], op=ALU.mult)

        def add_up(i):
            for m in range(TILES):
                for j, (t, func) in enumerate(((sq_re[i], ACT.Relu), (mu_g[i], ACT.Abs))):
                    nc.scalar.activation(out=t[:, m, :], in_=t[:, m, :], func=func, accum_out=sums[:, m, 2 * i + j:2 * i + j + 1])

        def add_up_mu(m):
            nc.scalar.activation(out=unused[:], in_=mu[:, m, :], func=ACT.Relu, scale=-1.0, accum_out=sums[:, m, 2 * PAIRS:2 * PAIRS + 1])

        y_units = [("y", c, h) for c in range(CHUNKS) for h in range(2)]
        order = [("im", VOLT, 0), ("im", VOLT, 1)]
        taken = 0
        for k in range(2 * CHUNKS):
            order.append(("im", k // 2, k % 2))
            if (k + 1) * Y_UNITS_EARLY // (2 * CHUNKS) > taken:
                order.append(y_units[taken])
                taken += 1
        order += y_units[taken:]
        step_of = {unit: s for s, unit in enumerate(order)}

        tensor_jobs, scalar_jobs, vector_jobs = {}, {}, {}

        def at(jobs, step, fn, *args):
            jobs.setdefault(step, []).append((fn, args))

        def do(jobs, step):
            for fn, args in jobs.get(step, []):
                fn(*args)

        for a, b in zip(FIRST_CUTS, FIRST_CUTS[1:]):
            for r in range(TILES):
                at(vector_jobs, -WIDEN_LEAD if b <= Y_HALF else 1 + r - WIDEN_LEAD, widen, 0, r, a, b)
        for c in range(1, CHUNKS - 1):
            for r in range(TILES):
                at(vector_jobs, step_of["y", c, 0] - WIDEN_LEAD + TILE_LAG * r, widen, c, r, 0, vector_cols(c))
        for h in range(2):
            for r in range(TILES):
                c = CHUNKS - 1
                at(vector_jobs, step_of["y", c, h] - WIDEN_LEAD + r, widen, c, r, h * Y_HALF, (h + 1) * Y_HALF)

        quantised = {}
        for c in range(VOLT, CHUNKS):
            done = step_of["im", c, 1] + QUANT_LAG
            if c == VOLT:
                at(vector_jobs, done - 1, quantise, "im", c, 0, IM_UNIT)
                at(vector_jobs, done, quantise, "im", c, IM_UNIT, PASSES_1)
            else:
                at(vector_jobs, done, quantise, "im", c, 0, PASSES_1)
            quantised["im", c] = done
        for c in range(CHUNKS - 1):
            done = step_of["y", c, 1] + QUANT_LAG
            at(vector_jobs, done, quantise, "y", c, 0, 4)
            at(vector_jobs, done, quantise, "y", c, 4, PASSES_2)
            quantised["y", c] = done
        c = CHUNKS - 1
        done = step_of["y", c, 1] + 1
        for h in range(2):
            at(vector_jobs, done, quantise, "y", c, 3 * h, 3 * h + 2)
            at(vector_jobs, done, quantise, "y", c, 3 * h + 2, 3 * h + 3)
        quantised["y", c] = done

        for c in range(CHUNKS):
            step = quantised["im", c] + 1
            at(tensor_jobs, step, multiply_1, c)
            if c % 2:
                at(scalar_jobs, step, empty_d, c // 2)
                at(vector_jobs, step + (D_LAG if c < CHUNKS - 1 else 1), quantise_d, c // 2)

        step, in_step = step + 2, 0
        for c in range(CHUNKS):
            ready = max(step, quantised["y", c] + 1)
            if c < CHUNKS - 1:
                for m in range(TILES):
                    at(tensor_jobs, ready, multiply_2, c, m, 0, PASSES_2)
            else:
                for a, b in ((0, PASSES_2 - 1), (PASSES_2 - 1, PASSES_2)):
                    for m in range(TILES):
                        at(tensor_jobs, ready, multiply_2, c, m, a, b)
            if c % 2 == 0:
                at(scalar_jobs, ready, square_re, c // 2)
                at(vector_jobs, ready + 1, subtract_limit, c // 2)
            elif c < CHUNKS - 1:
                at(scalar_jobs, ready, square_im, c // 2)
                at(vector_jobs, ready + 1, combine, c // 2, slice(0, TILES))
                at(scalar_jobs, ready + 2, add_up, c // 2)
            else:
                at(scalar_jobs, ready, square_im, c // 2)
                for m in range(TILES):
                    at(vector_jobs, ready, combine, c // 2, slice(m, m + 1))
                at(scalar_jobs, ready + 1, add_up, c // 2)
            in_step = in_step + 1 if ready == step else 1
            step = ready + in_step // 2
            in_step = in_step % 2
        steps = ready + 2

        for c in SCALAR_CHUNKS:
            at(scalar_jobs, step_of["y", c, 1] - CAST_LEAD, cast_last_pass, c)
        at(scalar_jobs, 12, load_limits)
        at(scalar_jobs, 20, square_limit)
        for m in range(TILES):
            at(scalar_jobs, 24 + 6 * m, add_up_mu, m)

        with tc.manual_schedule():
            nc.gpsimd.memset(totals[:], 0.0)
            nc.sync.dma_start(out=scale_k[:], in_=Ybr_scale.rearrange("o (g p t) -> p (o g) t", p=P, t=4))
            load_y(0)
            load_rows(VOLT)
            load_rows(0)
            load_y(1)
            load_rows(1)
            for g in range(PASSES_2):
                spread_scales(g)
            for step in range(-WIDEN_LEAD, steps):
                unit = order[step] if 0 <= step < len(order) else None
                if unit:
                    kind, c, h = unit
                    if h == 0 and 0 <= c < CHUNKS - 2:
                        if kind == "im":
                            load_rows(c + 2)
                        else:
                            load_y(c + 2)
                    turn(unit)
                do(tensor_jobs, step)
                if unit:
                    empty(unit)
                do(scalar_jobs, step)
                do(vector_jobs, step)

            nc.vector.tensor_reduce(out=totals[:, 0:TILES], in_=sums[:], axis=AX.X, op=ALU.add)
            bank = psum.tile([P, P], F32, name="sum", bufs=SUM_BANKS)
            nc.tensor.transpose(bank[:], totals[:], identity[:])
            nc.vector.tensor_copy(out=totals_t[:], in_=bank[:])
            nc.sync.dma_start(out=out.rearrange("(m p) -> m p", p=P), in_=totals_t[0:TILES, :])
